import numpy as np
import ml_dtypes


def mxq(x, axis, fmt="e4m3"):
    dtype, down = {"e4m3": (ml_dtypes.float8_e4m3fn, 7), "e5m2": (ml_dtypes.float8_e5m2, 14)}[fmt]
    v = np.moveaxis(np.asarray(x, np.float32).astype(ml_dtypes.bfloat16).astype(np.float64), axis, -1)
    blocks = v.reshape(v.shape[:-1] + (-1, 32))
    amax = np.abs(blocks).max(-1, keepdims=True)
    byte = np.maximum(np.where(amax > 0, np.frexp(amax)[1] - 1 + 127, 0) - down, 1)
    scale = np.exp2(byte - 127.0)
    codes = (blocks / scale).astype(np.float32).astype(dtype).astype(np.float64)
    return np.moveaxis((codes * scale).reshape(v.shape), -1, axis)


WIDE = False


def mx_kscale(k):
    if not WIDE:
        return np.ones(k)
    levels = np.array([10, -10, 5, -5, 0])
    a = np.random.permutation(np.resize(levels, k // 512 * 4)).reshape(k // 512, 4)
    idx = np.arange(k)
    return np.exp2(a[idx // 512, idx % 128 // 32])


BF16 = ml_dtypes.bfloat16


def bf(x):
    return np.asarray(x, np.float32).astype(BF16)


def f64(x):
    return np.asarray(x).astype(np.float64)


B, S, H, R, K, RK = 3, 128, 1024, 512, 128, 512
EPS = 1e-6


def normalize(x):
    n = np.sqrt((x * x).sum(-1, keepdims=True))
    return x / np.maximum(n, EPS)


def setup_inputs():
    s = mx_kscale(H)
    return {
        "hidden_states": bf((np.random.standard_normal((B, S, H)) + 0.5) * s),
        "Wr": bf(np.random.standard_normal((R, H)) / np.sqrt(H) / s),
        "scratch": bf(np.random.standard_normal((K, R))),
        "threshold": bf(5.0 + 0.5 * np.random.standard_normal(K)),
        "calib_mean": bf(0.5 * np.random.standard_normal(K) / np.sqrt(R)),
        "calib_std": bf((1.0 + 0.1 * np.random.standard_normal(K)) * 0.7 / np.sqrt(R)),
    }


def reference(hidden_states, Wr, scratch, threshold, calib_mean, calib_std):
    z = mxq(f64(hidden_states), 2, "e4m3") @ mxq(f64(Wr), 1, "e4m3").T
    z_norm = normalize(z)
    scratch_norm = normalize(f64(scratch))
    scores = mxq(z_norm, 2, "e4m3") @ mxq(scratch_norm, 1, "e4m3").T
    standardized = (scores - f64(calib_mean)) / np.maximum(f64(calib_std), EPS) - f64(threshold)
    logits = np.concatenate([standardized, np.zeros((B, S, 1))], axis=-1)
    e = np.exp(logits - logits.max(-1, keepdims=True))
    routing = e / e.sum(-1, keepdims=True)
    return scores, routing

@@ -1,0 +1,242 @@
+from contextlib import ExitStack
+
+import concourse.mybir as mybir
+from concourse.masks import make_identity
+
+F32 = mybir.dt.float32
+BF16 = mybir.dt.bfloat16
+U32 = mybir.dt.uint32
+U8 = mybir.dt.uint8
+FP8X4 = mybir.dt.float8_e4m3fn_x4
+ALU = mybir.AluOpType
+ACT = mybir.ActivationFunctionType
+AXIS = mybir.AxisListType
+
+P = 128
+PACK = 4
+K_PASS = P * PACK
+BATCH, TOKENS, HIDDEN = 3, 128, 1024
+RANK, MODES = 512, 128
+PASSES = HIDDEN // K_PASS
+WR_TILES = RANK // P
+WR_TILES_BEFORE_SCRATCH = 2
+PAIRS = 2
+EPS = 1e-6
+
+FLOPS = 2 * BATCH * TOKENS * HIDDEN * RANK + 2 * BATCH * TOKENS * RANK * MODES
+
+
+def tile_persistentcontrollayer_pa_s_kernel(
+    tc, hidden_states, Wr, scratch, threshold, calib_mean, calib_std, out_0, out_1
+):
+    nc = tc.nc
+    with ExitStack() as ctx:
+        keep = ctx.enter_context(tc.tile_pool(name="keep", bufs=1))
+        ps_turn = ctx.enter_context(tc.psum_pool(name="ps_turn", bufs=4))
+        ps_acc = ctx.enter_context(tc.psum_pool(name="ps_acc", bufs=1))
+        ps_cal = ctx.enter_context(tc.psum_pool(name="ps_cal", bufs=1))
+
+        scratch_sb = keep.tile([P, RANK], BF16, name="scratch_sb")
+        nc.sync.dma_start(out=scratch_sb[:], in_=scratch)
+        wr_rows = Wr.rearrange("(p t) k -> t p k", t=WR_TILES)
+        wr_sb = [keep.tile([P, HIDDEN], BF16, name="wr_sb%d" % t) for t in range(WR_TILES)]
+        for t in range(WR_TILES):
+            nc.sync.dma_start(out=wr_sb[t][:], in_=wr_rows[t])
+        hs_sb = [keep.tile([P, HIDDEN], BF16, name="hs_sb%d" % b) for b in range(BATCH)]
+        for b in range(BATCH):
+            nc.sync.dma_start(out=hs_sb[b][:], in_=hidden_states[b])
+
+        calib_rows = keep.tile([P, P], BF16, name="calib_rows")
+        nc.vector.memset(calib_rows[:], 0.0)
+        for row, vec in enumerate((calib_mean, calib_std, threshold)):
+            nc.scalar.dma_start(
+                out=calib_rows[row : row + 1, :], in_=vec.rearrange("(o m) -> o m", o=1)
+            )
+
+        ident_bf = keep.tile([P, P], BF16, name="ident_bf")
+        make_identity(nc, ident_bf[:])
+        ident_f32 = keep.tile([P, P], F32, name="ident_f32")
+        make_identity(nc, ident_f32[:])
+        neg_half = keep.tile([P, 1], F32, name="neg_half")
+        nc.gpsimd.memset(neg_half[:], -0.5)
+        logits = keep.tile([P, BATCH, MODES + 1], F32, name="logits")
+        nc.vector.memset(logits[:, :, MODES : MODES + 1], 0.0)
+
+        squares = keep.tile([P, RANK], BF16, name="squares")
+
+        def inverse_norm(values, c):
+            nc.scalar.activation(
+                out=squares[:], in_=values, func=ACT.Square, accum_out=sum_sq[:, c : c + 1]
+            )
+            nc.gpsimd.tensor_scalar(
+                out=clamped[:, c : c + 1], in0=sum_sq[:, c : c + 1], scalar1=EPS * EPS, scalar2=None,
+                op0=ALU.max,
+            )
+            nc.gpsimd.tensor_tensor(
+                out=inv_norm[:, c : c + 1], in0=clamped[:, c : c + 1], in1=neg_half[:], op=ALU.pow
+            )
+
+        calib_ps = ps_cal.tile([P, P], BF16, tag="cal", name="calib_ps")
+        nc.tensor.transpose(out=calib_ps[:], in_=calib_rows[:], identity=ident_bf[:])
+        calib = keep.tile([P, 3], F32, name="calib")
+        nc.vector.tensor_copy(out=calib[:], in_=calib_ps[:, 0:3])
+        std_floor = keep.tile([P, 1], F32, name="std_floor")
+        nc.vector.tensor_scalar_max(out=std_floor[:], in0=calib[:, 1:2], scalar1=EPS)
+        affine = keep.tile([P, 2], F32, name="affine")
+        nc.vector.reciprocal(out=affine[:, 0:1], in_=std_floor[:])
+        nc.vector.tensor_scalar(
+            out=affine[:, 1:2], in0=calib[:, 0:1], scalar1=affine[:, 0:1], scalar2=calib[:, 2:3],
+            op0=ALU.mult, op1=ALU.add,
+        )
+
+        sum_sq = keep.tile([P, 1 + BATCH], F32, name="sum_sq")
+        clamped = keep.tile([P, 1 + BATCH], F32, name="clamped")
+        inv_norm = keep.tile([P, 1 + BATCH], F32, name="inv_norm")
+        inverse_norm(scratch_sb[:], 0)
+        s_norm = keep.tile([P, PACK, P], BF16, name="s_norm")
+        nc.vector.tensor_scalar(
+            out=s_norm[:], in0=scratch_sb[:].rearrange("m (p t) -> m t p", t=PACK),
+            scalar1=inv_norm[:, 0:1], scalar2=None, op0=ALU.mult,
+        )
+
+        spread_ps = ps_cal.tile([P, 2, P], F32, tag="cal", name="spread_ps")
+        for c in range(2):
+            nc.tensor.matmul(
+                out=spread_ps[:, c, :], lhsT=affine[:, c : c + 1].to_broadcast([P, P]),
+                rhs=ident_f32[:], start=True, stop=True,
+            )
+        spread = keep.tile([P, 2, P], F32, name="spread")
+        nc.vector.tensor_copy(out=spread[:], in_=spread_ps[:])
+
+        def turn_rows(rows_sb, grouped_words):
+            words = rows_sb[:].bitcast(F32)
+            turned = ps_turn.tile([P, PASSES, PAIRS, P], F32, tag="turn", name="turned")
+            for g in range(PASSES):
+                for u in range(PAIRS):
+                    first = (g * PAIRS + u) * P
+                    nc.tensor.transpose(
+                        out=turned[:, g, u, :], in_=words[:, first : first + P], identity=ident_f32[:]
+                    )
+            nc.scalar.copy(out=grouped_words, in_=turned[:].rearrange("p g u r -> p g r u"))
+
+        wr_grouped = keep.tile([P, PASSES * RANK * PACK], BF16, name="wr_grouped", align_bytes=64)
+        wr_codes = keep.tile([P, PASSES * RANK], U32, name="wr_codes", align_bytes=64)
+        wr_scales = keep.tile([P, PASSES * RANK], U8, name="wr_scales", align_bytes=64)
+        wr_words = wr_grouped[:].bitcast(F32).rearrange(
+            "p (g t r u) -> p g t r u", g=PASSES, t=WR_TILES, u=PAIRS
+        )
+
+        def quantise_wr(t):
+            turn_rows(wr_sb[t], wr_words[:, :, t])
+            for g in range(PASSES):
+                first = (g * WR_TILES + t) * P
+                nc.vector.quantize_mx(
+                    out=wr_codes[:, first : first + P].bitcast(FP8X4),
+                    scales=wr_scales[:, first : first + P],
+                    in_=wr_grouped[:, first * PACK : (first + P) * PACK],
+                )
+
+        s_grouped = keep.tile([P, MODES, PACK], BF16, name="s_grouped", align_bytes=64)
+        s_codes = keep.tile([P, MODES], U32, name="s_codes", align_bytes=64)
+        s_scales = keep.tile([P, MODES], U8, name="s_scales", align_bytes=64)
+
+        def turn_and_quantise(normed, grouped, codes, scales):
+            turned = ps_turn.tile([P, PACK, P], BF16, tag="turn", name="turned_bf")
+            for t in range(PACK):
+                nc.tensor.transpose(out=turned[:, t, :], in_=normed[:, t, :], identity=ident_bf[:])
+            nc.scalar.copy(out=grouped, in_=turned[:].rearrange("p t r -> p r t"))
+            nc.vector.quantize_mx(
+                out=codes.bitcast(FP8X4), scales=scales, in_=grouped.rearrange("p r t -> p (r t)")
+            )
+
+        for t in range(WR_TILES):
+            if t == WR_TILES_BEFORE_SCRATCH:
+                turn_and_quantise(s_norm, s_grouped[:], s_codes[:], s_scales[:])
+            quantise_wr(t)
+
+        hs_grouped = [
+            keep.tile([P, PASSES * TOKENS * PACK], BF16, name="hs_grouped%d" % b, align_bytes=64)
+            for b in range(BATCH)
+        ]
+        hs_codes = [
+            keep.tile([P, PASSES * TOKENS], U32, name="hs_codes%d" % b, align_bytes=64)
+            for b in range(BATCH)
+        ]
+        hs_scales = [
+            keep.tile([P, PASSES * TOKENS], U8, name="hs_scales%d" % b, align_bytes=64)
+            for b in range(BATCH)
+        ]
+        for b in range(BATCH):
+            turn_rows(
+                hs_sb[b],
+                hs_grouped[b][:].bitcast(F32).rearrange("p (g r u) -> p g r u", g=PASSES, u=PAIRS),
+            )
+            nc.vector.quantize_mx(
+                out=hs_codes[b][:].bitcast(FP8X4), scales=hs_scales[b][:], in_=hs_grouped[b][:]
+            )
+
+        z_ps = []
+        for b in range(BATCH):
+            z_ps.append(ps_acc.tile([P, RANK], F32, tag="acc%d" % b, name="z_ps%d" % b))
+            for g in range(PASSES):
+                nc.tensor.matmul_mx(
+                    out=z_ps[b][:],
+                    lhsT=hs_codes[b][:, g * TOKENS : (g + 1) * TOKENS].bitcast(FP8X4),
+                    lhsT_scale=hs_scales[b][:, g * TOKENS : (g + 1) * TOKENS],
+                    rhs=wr_codes[:, g * RANK : (g + 1) * RANK].bitcast(FP8X4),
+                    rhs_scale=wr_scales[:, g * RANK : (g + 1) * RANK],
+                    start=(g == 0),
+                    stop=(g == PASSES - 1),
+                )
+            inverse_norm(z_ps[b][:], 1 + b)
+
+        z_norm = keep.tile([P, BATCH, PACK, P], BF16, name="z_norm")
+        z_grouped = keep.tile([P, BATCH, TOKENS, PACK], BF16, name="z_grouped", align_bytes=64)
+        z_codes = keep.tile([P, BATCH, TOKENS], U32, name="z_codes", align_bytes=64)
+        z_scales = keep.tile([P, BATCH, TOKENS], U8, name="z_scales", align_bytes=64)
+        scores_sb = keep.tile([P, BATCH, MODES], F32, name="scores_sb")
+        scaled = keep.tile([P, BATCH, MODES], F32, name="scaled")
+        neg_max = keep.tile([P, BATCH], F32, name="neg_max")
+        expd = keep.tile([P, BATCH, MODES + 1], F32, name="expd")
+        exp_sum = keep.tile([P, BATCH], F32, name="exp_sum")
+        inv_sum = keep.tile([P, BATCH], F32, name="inv_sum")
+        routing = keep.tile([P, BATCH, MODES + 1], F32, name="routing")
+
+        for b in range(BATCH):
+            nc.vector.tensor_scalar(
+                out=z_norm[:, b].rearrange("k t p -> k (t p)"), in0=z_ps[b][:],
+                scalar1=inv_norm[:, 1 + b : 2 + b], scalar2=None, op0=ALU.mult,
+            )
+        for b in range(BATCH):
+            turn_and_quantise(z_norm[:, b], z_grouped[:, b], z_codes[:, b, :], z_scales[:, b, :])
+
+        for b in range(BATCH):
+            for_logits = ps_acc.tile([P, MODES], F32, tag="acc%d" % b, name="for_logits")
+            for_store = ps_turn.tile([P, MODES], F32, tag="turn", name="for_store")
+            for bank in (for_logits, for_store):
+                nc.tensor.matmul_mx(
+                    out=bank[:],
+                    lhsT=z_codes[:, b, :].bitcast(FP8X4), lhsT_scale=z_scales[:, b, :],
+                    rhs=s_codes[:].bitcast(FP8X4), rhs_scale=s_scales[:],
+                    start=True, stop=True,
+                )
+            nc.scalar.copy(out=scores_sb[:, b, :], in_=for_store[:])
+            nc.sync.dma_start(out=out_0[b], in_=scores_sb[:, b, :])
+            nc.vector.tensor_tensor(
+                out=scaled[:, b, :], in0=for_logits[:], in1=spread[:, 0, :], op=ALU.mult
+            )
+            nc.vector.tensor_tensor(
+                out=logits[:, b, 0:MODES], in0=scaled[:, b, :], in1=spread[:, 1, :], op=ALU.subtract
+            )
+            nc.vector.tensor_reduce(
+                out=neg_max[:, b : b + 1], in_=logits[:, b, :], axis=AXIS.X, op=ALU.max, negate=True
+            )
+            nc.scalar.activation(
+                out=expd[:, b, :], in_=logits[:, b, :], func=ACT.Exp,
+                bias=neg_max[:, b : b + 1], scale=1.0, accum_out=exp_sum[:, b : b + 1],
+            )
+            nc.vector.reciprocal(out=inv_sum[:, b : b + 1], in_=exp_sum[:, b : b + 1])
+            nc.scalar.activation(
+                out=routing[:, b, :], in_=expd[:, b, :], func=ACT.Copy, scale=inv_sum[:, b : b + 1]
+            )
+            nc.sync.dma_start(out=out_1[b], in_=routing[:, b, :])

@@ -19,7 +19,6 @@ BATCH, TOKENS, HIDDEN = 3, 128, 1024
 RANK, MODES = 512, 128
 PASSES = HIDDEN // K_PASS
 WR_TILES = RANK // P
-WR_TILES_BEFORE_SCRATCH = 2
 PAIRS = 2
 EPS = 1e-6
 
@@ -35,34 +34,55 @@ def tile_persistentcontrollayer_pa_s_kernel(
         ps_turn = ctx.enter_context(tc.psum_pool(name="ps_turn", bufs=4))
         ps_acc = ctx.enter_context(tc.psum_pool(name="ps_acc", bufs=1))
         ps_cal = ctx.enter_context(tc.psum_pool(name="ps_cal", bufs=1))
+        ctx.enter_context(tc.manual_schedule())
 
         scratch_sb = keep.tile([P, RANK], BF16, name="scratch_sb")
-        nc.sync.dma_start(out=scratch_sb[:], in_=scratch)
-        wr_rows = Wr.rearrange("(p t) k -> t p k", t=WR_TILES)
         wr_sb = [keep.tile([P, HIDDEN], BF16, name="wr_sb%d" % t) for t in range(WR_TILES)]
-        for t in range(WR_TILES):
-            nc.sync.dma_start(out=wr_sb[t][:], in_=wr_rows[t])
         hs_sb = [keep.tile([P, HIDDEN], BF16, name="hs_sb%d" % b) for b in range(BATCH)]
-        for b in range(BATCH):
-            nc.sync.dma_start(out=hs_sb[b][:], in_=hidden_states[b])
-
         calib_rows = keep.tile([P, P], BF16, name="calib_rows")
-        nc.vector.memset(calib_rows[:], 0.0)
-        for row, vec in enumerate((calib_mean, calib_std, threshold)):
-            nc.scalar.dma_start(
-                out=calib_rows[row : row + 1, :], in_=vec.rearrange("(o m) -> o m", o=1)
-            )
-
         ident_bf = keep.tile([P, P], BF16, name="ident_bf")
-        make_identity(nc, ident_bf[:])
         ident_f32 = keep.tile([P, P], F32, name="ident_f32")
-        make_identity(nc, ident_f32[:])
         neg_half = keep.tile([P, 1], F32, name="neg_half")
-        nc.gpsimd.memset(neg_half[:], -0.5)
-        logits = keep.tile([P, BATCH, MODES + 1], F32, name="logits")
-        nc.vector.memset(logits[:, :, MODES : MODES + 1], 0.0)
-
         squares = keep.tile([P, RANK], BF16, name="squares")
+        sum_sq = keep.tile([P, 1 + BATCH], F32, name="sum_sq")
+        clamped = keep.tile([P, 1 + BATCH], F32, name="clamped")
+        inv_norm = keep.tile([P, 1 + BATCH], F32, name="inv_norm")
+        calib = keep.tile([P, 3], F32, name="calib")
+        std_floor = keep.tile([P, 1], F32, name="std_floor")
+        affine = keep.tile([P, 2], F32, name="affine")
+        repeated = keep.tile([P, 2, P], F32, name="repeated")
+        spread = keep.tile([P, 2, P], F32, name="spread")
+        s_norm = keep.tile([P, PACK, P], BF16, name="s_norm")
+        s_grouped = keep.tile([P, MODES, PACK], BF16, name="s_grouped", align_bytes=64)
+        s_codes = keep.tile([P, MODES], U32, name="s_codes", align_bytes=64)
+        s_scales = keep.tile([P, MODES], U8, name="s_scales", align_bytes=64)
+        wr_grouped = keep.tile([P, PASSES * RANK * PACK], BF16, name="wr_grouped", align_bytes=64)
+        wr_codes = keep.tile([P, PASSES * RANK], U32, name="wr_codes", align_bytes=64)
+        wr_scales = keep.tile([P, PASSES * RANK], U8, name="wr_scales", align_bytes=64)
+        hs_grouped = [
+            keep.tile([P, PASSES * TOKENS * PACK], BF16, name="hs_grouped%d" % b, align_bytes=64)
+            for b in range(BATCH)
+        ]
+        hs_codes = [
+            keep.tile([P, PASSES * TOKENS], U32, name="hs_codes%d" % b, align_bytes=64)
+            for b in range(BATCH)
+        ]
+        hs_scales = [
+            keep.tile([P, PASSES * TOKENS], U8, name="hs_scales%d" % b, align_bytes=64)
+            for b in range(BATCH)
+        ]
+        z_norm = keep.tile([P, BATCH, PACK, P], BF16, name="z_norm")
+        z_grouped = keep.tile([P, BATCH, TOKENS, PACK], BF16, name="z_grouped", align_bytes=64)
+        z_codes = keep.tile([P, BATCH, TOKENS], U32, name="z_codes", align_bytes=64)
+        z_scales = keep.tile([P, BATCH, TOKENS], U8, name="z_scales", align_bytes=64)
+        scores_sb = keep.tile([P, BATCH, MODES], F32, name="scores_sb")
+        scaled = keep.tile([P, BATCH, MODES], F32, name="scaled")
+        logits = keep.tile([P, BATCH, MODES + 1], F32, name="logits")
+        neg_max = keep.tile([P, BATCH], F32, name="neg_max")
+        expd = keep.tile([P, BATCH, MODES + 1], F32, name="expd")
+        exp_sum = keep.tile([P, BATCH], F32, name="exp_sum")
+        inv_sum = keep.tile([P, BATCH], F32, name="inv_sum")
+        routing = keep.tile([P, BATCH, MODES + 1], F32, name="routing")
 
         def inverse_norm(values, c):
             nc.scalar.activation(
@@ -76,38 +96,6 @@ def tile_persistentcontrollayer_pa_s_kernel(
                 out=inv_norm[:, c : c + 1], in0=clamped[:, c : c + 1], in1=neg_half[:], op=ALU.pow
             )
 
-        calib_ps = ps_cal.tile([P, P], BF16, tag="cal", name="calib_ps")
-        nc.tensor.transpose(out=calib_ps[:], in_=calib_rows[:], identity=ident_bf[:])
-        calib = keep.tile([P, 3], F32, name="calib")
-        nc.vector.tensor_copy(out=calib[:], in_=calib_ps[:, 0:3])
-        std_floor = keep.tile([P, 1], F32, name="std_floor")
-        nc.vector.tensor_scalar_max(out=std_floor[:], in0=calib[:, 1:2], scalar1=EPS)
-        affine = keep.tile([P, 2], F32, name="affine")
-        nc.vector.reciprocal(out=affine[:, 0:1], in_=std_floor[:])
-        nc.vector.tensor_scalar(
-            out=affine[:, 1:2], in0=calib[:, 0:1], scalar1=affine[:, 0:1], scalar2=calib[:, 2:3],
-            op0=ALU.mult, op1=ALU.add,
-        )
-
-        sum_sq = keep.tile([P, 1 + BATCH], F32, name="sum_sq")
-        clamped = keep.tile([P, 1 + BATCH], F32, name="clamped")
-        inv_norm = keep.tile([P, 1 + BATCH], F32, name="inv_norm")
-        inverse_norm(scratch_sb[:], 0)
-        s_norm = keep.tile([P, PACK, P], BF16, name="s_norm")
-        nc.vector.tensor_scalar(
-            out=s_norm[:], in0=scratch_sb[:].rearrange("m (p t) -> m t p", t=PACK),
-            scalar1=inv_norm[:, 0:1], scalar2=None, op0=ALU.mult,
-        )
-
-        spread_ps = ps_cal.tile([P, 2, P], F32, tag="cal", name="spread_ps")
-        for c in range(2):
-            nc.tensor.matmul(
-                out=spread_ps[:, c, :], lhsT=affine[:, c : c + 1].to_broadcast([P, P]),
-                rhs=ident_f32[:], start=True, stop=True,
-            )
-        spread = keep.tile([P, 2, P], F32, name="spread")
-        nc.vector.tensor_copy(out=spread[:], in_=spread_ps[:])
-
         def turn_rows(rows_sb, grouped_words):
             words = rows_sb[:].bitcast(F32)
             turned = ps_turn.tile([P, PASSES, PAIRS, P], F32, tag="turn", name="turned")
@@ -119,9 +107,6 @@ def tile_persistentcontrollayer_pa_s_kernel(
                     )
             nc.scalar.copy(out=grouped_words, in_=turned[:].rearrange("p g u r -> p g r u"))
 
-        wr_grouped = keep.tile([P, PASSES * RANK * PACK], BF16, name="wr_grouped", align_bytes=64)
-        wr_codes = keep.tile([P, PASSES * RANK], U32, name="wr_codes", align_bytes=64)
-        wr_scales = keep.tile([P, PASSES * RANK], U8, name="wr_scales", align_bytes=64)
         wr_words = wr_grouped[:].bitcast(F32).rearrange(
             "p (g t r u) -> p g t r u", g=PASSES, t=WR_TILES, u=PAIRS
         )
@@ -136,37 +121,7 @@ def tile_persistentcontrollayer_pa_s_kernel(
                     in_=wr_grouped[:, first * PACK : (first + P) * PACK],
                 )
 
-        s_grouped = keep.tile([P, MODES, PACK], BF16, name="s_grouped", align_bytes=64)
-        s_codes = keep.tile([P, MODES], U32, name="s_codes", align_bytes=64)
-        s_scales = keep.tile([P, MODES], U8, name="s_scales", align_bytes=64)
-
-        def turn_and_quantise(normed, grouped, codes, scales):
-            turned = ps_turn.tile([P, PACK, P], BF16, tag="turn", name="turned_bf")
-            for t in range(PACK):
-                nc.tensor.transpose(out=turned[:, t, :], in_=normed[:, t, :], identity=ident_bf[:])
-            nc.scalar.copy(out=grouped, in_=turned[:].rearrange("p t r -> p r t"))
-            nc.vector.quantize_mx(
-                out=codes.bitcast(FP8X4), scales=scales, in_=grouped.rearrange("p r t -> p (r t)")
-            )
-
-        for t in range(WR_TILES):
-            if t == WR_TILES_BEFORE_SCRATCH:
-                turn_and_quantise(s_norm, s_grouped[:], s_codes[:], s_scales[:])
-            quantise_wr(t)
-
-        hs_grouped = [
-            keep.tile([P, PASSES * TOKENS * PACK], BF16, name="hs_grouped%d" % b, align_bytes=64)
-            for b in range(BATCH)
-        ]
-        hs_codes = [
-            keep.tile([P, PASSES * TOKENS], U32, name="hs_codes%d" % b, align_bytes=64)
-            for b in range(BATCH)
-        ]
-        hs_scales = [
-            keep.tile([P, PASSES * TOKENS], U8, name="hs_scales%d" % b, align_bytes=64)
-            for b in range(BATCH)
-        ]
-        for b in range(BATCH):
+        def quantise_hs(b):
             turn_rows(
                 hs_sb[b],
                 hs_grouped[b][:].bitcast(F32).rearrange("p (g r u) -> p g r u", g=PASSES, u=PAIRS),
@@ -175,8 +130,38 @@ def tile_persistentcontrollayer_pa_s_kernel(
                 out=hs_codes[b][:].bitcast(FP8X4), scales=hs_scales[b][:], in_=hs_grouped[b][:]
             )
 
+        def turn_normed(normed, grouped):
+            turned = ps_turn.tile([P, PACK, P], BF16, tag="turn", name="turned_bf")
+            for t in range(PACK):
+                nc.tensor.transpose(out=turned[:, t, :], in_=normed[:, t, :], identity=ident_bf[:])
+            nc.scalar.copy(out=grouped, in_=turned[:].rearrange("p t r -> p r t"))
+
+        def quantise_normed(grouped, codes, scales):
+            nc.vector.quantize_mx(
+                out=codes.bitcast(FP8X4), scales=scales, in_=grouped.rearrange("p r t -> p (r t)")
+            )
+
+        def calib_columns():
+            calib_ps = ps_cal.tile([P, P], BF16, tag="cal", name="calib_ps")
+            nc.tensor.transpose(out=calib_ps[:], in_=calib_rows[:], identity=ident_bf[:])
+            nc.vector.tensor_copy(out=calib[:], in_=calib_ps[:, 0:3])
+            nc.vector.tensor_scalar_max(out=std_floor[:], in0=calib[:, 1:2], scalar1=EPS)
+            nc.vector.reciprocal(out=affine[:, 0:1], in_=std_floor[:])
+            nc.vector.tensor_scalar(
+                out=affine[:, 1:2], in0=calib[:, 0:1], scalar1=affine[:, 0:1], scalar2=calib[:, 2:3],
+                op0=ALU.mult, op1=ALU.add,
+            )
+            nc.vector.tensor_copy(out=repeated[:], in_=affine[:].unsqueeze(2).to_broadcast([P, 2, P]))
+
+        def calib_spread():
+            spread_ps = ps_cal.tile([P, 2, P], F32, tag="cal", name="spread_ps")
+            for c in range(2):
+                nc.tensor.transpose(out=spread_ps[:, c, :], in_=repeated[:, c, :], identity=ident_f32[:])
+            nc.vector.tensor_copy(out=spread[:], in_=spread_ps[:])
+
         z_ps = []
-        for b in range(BATCH):
+
+        def first_matmul(b):
             z_ps.append(ps_acc.tile([P, RANK], F32, tag="acc%d" % b, name="z_ps%d" % b))
             for g in range(PASSES):
                 nc.tensor.matmul_mx(
@@ -188,32 +173,13 @@ def tile_persistentcontrollayer_pa_s_kernel(
                     start=(g == 0),
                     stop=(g == PASSES - 1),
                 )
-            inverse_norm(z_ps[b][:], 1 + b)
 
-        z_norm = keep.tile([P, BATCH, PACK, P], BF16, name="z_norm")
-        z_grouped = keep.tile([P, BATCH, TOKENS, PACK], BF16, name="z_grouped", align_bytes=64)
-        z_codes = keep.tile([P, BATCH, TOKENS], U32, name="z_codes", align_bytes=64)
-        z_scales = keep.tile([P, BATCH, TOKENS], U8, name="z_scales", align_bytes=64)
-        scores_sb = keep.tile([P, BATCH, MODES], F32, name="scores_sb")
-        scaled = keep.tile([P, BATCH, MODES], F32, name="scaled")
-        neg_max = keep.tile([P, BATCH], F32, name="neg_max")
-        expd = keep.tile([P, BATCH, MODES + 1], F32, name="expd")
-        exp_sum = keep.tile([P, BATCH], F32, name="exp_sum")
-        inv_sum = keep.tile([P, BATCH], F32, name="inv_sum")
-        routing = keep.tile([P, BATCH, MODES + 1], F32, name="routing")
+        for_logits = []
 
-        for b in range(BATCH):
-            nc.vector.tensor_scalar(
-                out=z_norm[:, b].rearrange("k t p -> k (t p)"), in0=z_ps[b][:],
-                scalar1=inv_norm[:, 1 + b : 2 + b], scalar2=None, op0=ALU.mult,
-            )
-        for b in range(BATCH):
-            turn_and_quantise(z_norm[:, b], z_grouped[:, b], z_codes[:, b, :], z_scales[:, b, :])
-
-        for b in range(BATCH):
-            for_logits = ps_acc.tile([P, MODES], F32, tag="acc%d" % b, name="for_logits")
+        def second_matmul(b):
+            for_logits.append(ps_acc.tile([P, MODES], F32, tag="acc%d" % b, name="for_logits%d" % b))
             for_store = ps_turn.tile([P, MODES], F32, tag="turn", name="for_store")
-            for bank in (for_logits, for_store):
+            for bank in (for_logits[b], for_store):
                 nc.tensor.matmul_mx(
                     out=bank[:],
                     lhsT=z_codes[:, b, :].bitcast(FP8X4), lhsT_scale=z_scales[:, b, :],
@@ -222,8 +188,10 @@ def tile_persistentcontrollayer_pa_s_kernel(
                 )
             nc.scalar.copy(out=scores_sb[:, b, :], in_=for_store[:])
             nc.sync.dma_start(out=out_0[b], in_=scores_sb[:, b, :])
+
+        def exponentials(b):
             nc.vector.tensor_tensor(
-                out=scaled[:, b, :], in0=for_logits[:], in1=spread[:, 0, :], op=ALU.mult
+                out=scaled[:, b, :], in0=for_logits[b][:], in1=spread[:, 0, :], op=ALU.mult
             )
             nc.vector.tensor_tensor(
                 out=logits[:, b, 0:MODES], in0=scaled[:, b, :], in1=spread[:, 1, :], op=ALU.subtract
@@ -235,8 +203,60 @@ def tile_persistentcontrollayer_pa_s_kernel(
                 out=expd[:, b, :], in_=logits[:, b, :], func=ACT.Exp,
                 bias=neg_max[:, b : b + 1], scale=1.0, accum_out=exp_sum[:, b : b + 1],
             )
+
+        def normalise(b):
             nc.vector.reciprocal(out=inv_sum[:, b : b + 1], in_=exp_sum[:, b : b + 1])
             nc.scalar.activation(
                 out=routing[:, b, :], in_=expd[:, b, :], func=ACT.Copy, scale=inv_sum[:, b : b + 1]
             )
             nc.sync.dma_start(out=out_1[b], in_=routing[:, b, :])
+
+        nc.sync.dma_start(out=scratch_sb[:], in_=scratch)
+        wr_rows = Wr.rearrange("(p t) k -> t p k", t=WR_TILES)
+        for t in range(WR_TILES):
+            nc.sync.dma_start(out=wr_sb[t][:], in_=wr_rows[t])
+        for b in range(BATCH):
+            nc.sync.dma_start(out=hs_sb[b][:], in_=hidden_states[b])
+        nc.vector.memset(calib_rows[:], 0.0)
+        for row, vec in enumerate((calib_mean, calib_std, threshold)):
+            nc.scalar.dma_start(
+                out=calib_rows[row : row + 1, :], in_=vec.rearrange("(o m) -> o m", o=1)
+            )
+        make_identity(nc, ident_f32[:])
+        make_identity(nc, ident_bf[:])
+        nc.gpsimd.memset(neg_half[:], -0.5)
+        nc.vector.memset(logits[:, :, MODES : MODES + 1], 0.0)
+
+        inverse_norm(scratch_sb[:], 0)
+        quantise_wr(0)
+        nc.vector.tensor_scalar(
+            out=s_norm[:], in0=scratch_sb[:].rearrange("m (p t) -> m t p", t=PACK),
+            scalar1=inv_norm[:, 0:1], scalar2=None, op0=ALU.mult,
+        )
+        quantise_wr(1)
+        calib_columns()
+        turn_normed(s_norm, s_grouped[:])
+        quantise_normed(s_grouped[:], s_codes[:], s_scales[:])
+        quantise_wr(2)
+        calib_spread()
+        quantise_wr(3)
+
+        for b in range(BATCH):
+            quantise_hs(b)
+        for b in range(BATCH):
+            first_matmul(b)
+            inverse_norm(z_ps[b][:], 1 + b)
+        for b in range(BATCH):
+            nc.vector.tensor_scalar(
+                out=z_norm[:, b].rearrange("k t p -> k (t p)"), in0=z_ps[b][:],
+                scalar1=inv_norm[:, 1 + b : 2 + b], scalar2=None, op0=ALU.mult,
+            )
+            turn_normed(z_norm[:, b], z_grouped[:, b])
+        for step in range(BATCH + 2):
+            if step < BATCH:
+                quantise_normed(z_grouped[:, step], z_codes[:, step, :], z_scales[:, step, :])
+                second_matmul(step)
+            if 1 <= step <= BATCH:
+                exponentials(step - 1)
+            if step >= 2:
+                normalise(step - 2)

@@ -31,7 +31,7 @@ def tile_persistentcontrollayer_pa_s_kernel(
     nc = tc.nc
     with ExitStack() as ctx:
         keep = ctx.enter_context(tc.tile_pool(name="keep", bufs=1))
-        ps_turn = ctx.enter_context(tc.psum_pool(name="ps_turn", bufs=4))
+        ps_turn = ctx.enter_context(tc.psum_pool(name="ps_turn", bufs=3))
         ps_acc = ctx.enter_context(tc.psum_pool(name="ps_acc", bufs=1))
         ps_cal = ctx.enter_context(tc.psum_pool(name="ps_cal", bufs=1))
         ctx.enter_context(tc.manual_schedule())
@@ -153,10 +153,13 @@ def tile_persistentcontrollayer_pa_s_kernel(
             )
             nc.vector.tensor_copy(out=repeated[:], in_=affine[:].unsqueeze(2).to_broadcast([P, 2, P]))
 
-        def calib_spread():
-            spread_ps = ps_cal.tile([P, 2, P], F32, tag="cal", name="spread_ps")
+        spread_ps = ps_cal.tile([P, 2, P], F32, tag="spread", name="spread_ps")
+
+        def calib_spread_turn():
             for c in range(2):
                 nc.tensor.transpose(out=spread_ps[:, c, :], in_=repeated[:, c, :], identity=ident_f32[:])
+
+        def calib_spread_copy():
             nc.vector.tensor_copy(out=spread[:], in_=spread_ps[:])
 
         z_ps = []
@@ -206,8 +209,9 @@ def tile_persistentcontrollayer_pa_s_kernel(
 
         def normalise(b):
             nc.vector.reciprocal(out=inv_sum[:, b : b + 1], in_=exp_sum[:, b : b + 1])
-            nc.scalar.activation(
-                out=routing[:, b, :], in_=expd[:, b, :], func=ACT.Copy, scale=inv_sum[:, b : b + 1]
+            nc.vector.tensor_scalar(
+                out=routing[:, b, :], in0=expd[:, b, :], scalar1=inv_sum[:, b : b + 1], scalar2=None,
+                op0=ALU.mult,
             )
             nc.sync.dma_start(out=out_1[b], in_=routing[:, b, :])
 
@@ -228,35 +232,38 @@ def tile_persistentcontrollayer_pa_s_kernel(
         nc.vector.memset(logits[:, :, MODES : MODES + 1], 0.0)
 
         inverse_norm(scratch_sb[:], 0)
-        quantise_wr(0)
         nc.vector.tensor_scalar(
             out=s_norm[:], in0=scratch_sb[:].rearrange("m (p t) -> m t p", t=PACK),
             scalar1=inv_norm[:, 0:1], scalar2=None, op0=ALU.mult,
         )
-        quantise_wr(1)
+        quantise_wr(0)
         calib_columns()
-        turn_normed(s_norm, s_grouped[:])
-        quantise_normed(s_grouped[:], s_codes[:], s_scales[:])
-        quantise_wr(2)
-        calib_spread()
-        quantise_wr(3)
-
+        for t in range(1, WR_TILES):
+            quantise_wr(t)
         for b in range(BATCH):
             quantise_hs(b)
         for b in range(BATCH):
             first_matmul(b)
             inverse_norm(z_ps[b][:], 1 + b)
+
+        turn_normed(s_norm, s_grouped[:])
+        calib_spread_turn()
+
         for b in range(BATCH):
             nc.vector.tensor_scalar(
                 out=z_norm[:, b].rearrange("k t p -> k (t p)"), in0=z_ps[b][:],
                 scalar1=inv_norm[:, 1 + b : 2 + b], scalar2=None, op0=ALU.mult,
             )
             turn_normed(z_norm[:, b], z_grouped[:, b])
-        for step in range(BATCH + 2):
-            if step < BATCH:
-                quantise_normed(z_grouped[:, step], z_codes[:, step, :], z_scales[:, step, :])
-                second_matmul(step)
-            if 1 <= step <= BATCH:
-                exponentials(step - 1)
-            if step >= 2:
-                normalise(step - 2)
+            if b == BATCH - 2:
+                calib_spread_copy()
+                quantise_normed(s_grouped[:], s_codes[:], s_scales[:])
+
+        for b in range(BATCH):
+            quantise_normed(z_grouped[:, b], z_codes[:, b, :], z_scales[:, b, :])
+            second_matmul(b)
+            if b >= 1:
+                exponentials(b - 1)
+        exponentials(BATCH - 1)
+        for b in range(BATCH):
+            normalise(b)

@@ -44,9 +44,9 @@ def tile_persistentcontrollayer_pa_s_kernel(
         ident_f32 = keep.tile([P, P], F32, name="ident_f32")
         neg_half = keep.tile([P, 1], F32, name="neg_half")
         squares = keep.tile([P, RANK], BF16, name="squares")
-        sum_sq = keep.tile([P, 1 + BATCH], F32, name="sum_sq")
-        clamped = keep.tile([P, 1 + BATCH], F32, name="clamped")
-        inv_norm = keep.tile([P, 1 + BATCH], F32, name="inv_norm")
+        sum_sq = [keep.tile([P, 1], F32, name="sum_sq%d" % c) for c in range(1 + BATCH)]
+        inv_root = [keep.tile([P, 1], F32, name="inv_root%d" % c) for c in range(1 + BATCH)]
+        inv_norm = [keep.tile([P, 1], F32, name="inv_norm%d" % c) for c in range(1 + BATCH)]
         calib = keep.tile([P, 3], F32, name="calib")
         std_floor = keep.tile([P, 1], F32, name="std_floor")
         affine = keep.tile([P, 2], F32, name="affine")
@@ -56,7 +56,10 @@ def tile_persistentcontrollayer_pa_s_kernel(
         s_grouped = keep.tile([P, MODES, PACK], BF16, name="s_grouped", align_bytes=64)
         s_codes = keep.tile([P, MODES], U32, name="s_codes", align_bytes=64)
         s_scales = keep.tile([P, MODES], U8, name="s_scales", align_bytes=64)
-        wr_grouped = keep.tile([P, PASSES * RANK * PACK], BF16, name="wr_grouped", align_bytes=64)
+        wr_grouped = [
+            keep.tile([P, PASSES * P * PACK], BF16, name="wr_grouped%d" % t, align_bytes=64)
+            for t in range(WR_TILES)
+        ]
         wr_codes = keep.tile([P, PASSES * RANK], U32, name="wr_codes", align_bytes=64)
         wr_scales = keep.tile([P, PASSES * RANK], U8, name="wr_scales", align_bytes=64)
         hs_grouped = [
@@ -84,16 +87,14 @@ def tile_persistentcontrollayer_pa_s_kernel(
         inv_sum = keep.tile([P, BATCH], F32, name="inv_sum")
         routing = keep.tile([P, BATCH, MODES + 1], F32, name="routing")
 
-        def inverse_norm(values, c):
-            nc.scalar.activation(
-                out=squares[:], in_=values, func=ACT.Square, accum_out=sum_sq[:, c : c + 1]
-            )
-            nc.gpsimd.tensor_scalar(
-                out=clamped[:, c : c + 1], in0=sum_sq[:, c : c + 1], scalar1=EPS * EPS, scalar2=None,
-                op0=ALU.max,
-            )
-            nc.gpsimd.tensor_tensor(
-                out=inv_norm[:, c : c + 1], in0=clamped[:, c : c + 1], in1=neg_half[:], op=ALU.pow
+        def inverse_root(values, c):
+            nc.scalar.activation(out=squares[:], in_=values, func=ACT.Square, accum_out=sum_sq[c][:])
+            nc.gpsimd.tensor_tensor(out=inv_root[c][:], in0=sum_sq[c][:], in1=neg_half[:], op=ALU.pow)
+
+        def normalise_rows(normed, values, c):
+            nc.vector.tensor_scalar_min(out=inv_norm[c][:], in0=inv_root[c][:], scalar1=1.0 / EPS)
+            nc.vector.tensor_scalar(
+                out=normed, in0=values, scalar1=inv_norm[c][:], scalar2=None, op0=ALU.mult
             )
 
         def turn_rows(rows_sb, grouped_words):
@@ -107,18 +108,17 @@ def tile_persistentcontrollayer_pa_s_kernel(
                     )
             nc.scalar.copy(out=grouped_words, in_=turned[:].rearrange("p g u r -> p g r u"))
 
-        wr_words = wr_grouped[:].bitcast(F32).rearrange(
-            "p (g t r u) -> p g t r u", g=PASSES, t=WR_TILES, u=PAIRS
-        )
-
         def quantise_wr(t):
-            turn_rows(wr_sb[t], wr_words[:, :, t])
+            turn_rows(
+                wr_sb[t],
+                wr_grouped[t][:].bitcast(F32).rearrange("p (g r u) -> p g r u", g=PASSES, u=PAIRS),
+            )
             for g in range(PASSES):
                 first = (g * WR_TILES + t) * P
                 nc.vector.quantize_mx(
                     out=wr_codes[:, first : first + P].bitcast(FP8X4),
                     scales=wr_scales[:, first : first + P],
-                    in_=wr_grouped[:, first * PACK : (first + P) * PACK],
+                    in_=wr_grouped[t][:, g * P * PACK : (g + 1) * P * PACK],
                 )
 
         def quantise_hs(b):
@@ -231,11 +231,8 @@ def tile_persistentcontrollayer_pa_s_kernel(
         nc.gpsimd.memset(neg_half[:], -0.5)
         nc.vector.memset(logits[:, :, MODES : MODES + 1], 0.0)
 
-        inverse_norm(scratch_sb[:], 0)
-        nc.vector.tensor_scalar(
-            out=s_norm[:], in0=scratch_sb[:].rearrange("m (p t) -> m t p", t=PACK),
-            scalar1=inv_norm[:, 0:1], scalar2=None, op0=ALU.mult,
-        )
+        inverse_root(scratch_sb[:], 0)
+        normalise_rows(s_norm[:], scratch_sb[:].rearrange("m (p t) -> m t p", t=PACK), 0)
         quantise_wr(0)
         calib_columns()
         for t in range(1, WR_TILES):
@@ -244,16 +241,13 @@ def tile_persistentcontrollayer_pa_s_kernel(
             quantise_hs(b)
         for b in range(BATCH):
             first_matmul(b)
-            inverse_norm(z_ps[b][:], 1 + b)
+            inverse_root(z_ps[b][:], 1 + b)
 
         turn_normed(s_norm, s_grouped[:])
         calib_spread_turn()
 
         for b in range(BATCH):
-            nc.vector.tensor_scalar(
-                out=z_norm[:, b].rearrange("k t p -> k (t p)"), in0=z_ps[b][:],
-                scalar1=inv_norm[:, 1 + b : 2 + b], scalar2=None, op0=ALU.mult,
-            )
+            normalise_rows(z_norm[:, b].rearrange("k t p -> k (t p)"), z_ps[b][:], 1 + b)
             turn_normed(z_norm[:, b], z_grouped[:, b])
             if b == BATCH - 2:
                 calib_spread_copy()

@@ -21,6 +21,7 @@ PASSES = HIDDEN // K_PASS
 WR_TILES = RANK // P
 PAIRS = 2
 EPS = 1e-6
+IDLE_MATMULS_AT_START = 3
 
 FLOPS = 2 * BATCH * TOKENS * HIDDEN * RANK + 2 * BATCH * TOKENS * RANK * MODES
 
@@ -34,6 +35,7 @@ def tile_persistentcontrollayer_pa_s_kernel(
         ps_turn = ctx.enter_context(tc.psum_pool(name="ps_turn", bufs=3))
         ps_acc = ctx.enter_context(tc.psum_pool(name="ps_acc", bufs=1))
         ps_cal = ctx.enter_context(tc.psum_pool(name="ps_cal", bufs=1))
+        ps_idle = ctx.enter_context(tc.psum_pool(name="ps_idle", bufs=1))
         ctx.enter_context(tc.manual_schedule())
 
         scratch_sb = keep.tile([P, RANK], BF16, name="scratch_sb")
@@ -87,6 +89,11 @@ def tile_persistentcontrollayer_pa_s_kernel(
         inv_sum = keep.tile([P, BATCH], F32, name="inv_sum")
         routing = keep.tile([P, BATCH, MODES + 1], F32, name="routing")
 
+        idle_ps = ps_idle.tile([P, P], F32, name="idle_ps")
+
+        def idle_matmul():
+            nc.tensor.matmul(out=idle_ps[:], lhsT=ident_f32[:], rhs=ident_f32[:], start=True, stop=True)
+
         def inverse_root(values, c):
             nc.scalar.activation(out=squares[:], in_=values, func=ACT.Square, accum_out=sum_sq[c][:])
             nc.gpsimd.tensor_tensor(out=inv_root[c][:], in0=sum_sq[c][:], in1=neg_half[:], op=ALU.pow)
@@ -106,6 +113,7 @@ def tile_persistentcontrollayer_pa_s_kernel(
                     nc.tensor.transpose(
                         out=turned[:, g, u, :], in_=words[:, first : first + P], identity=ident_f32[:]
                     )
+            idle_matmul()
             nc.scalar.copy(out=grouped_words, in_=turned[:].rearrange("p g u r -> p g r u"))
 
         def quantise_wr(t):
@@ -153,14 +161,17 @@ def tile_persistentcontrollayer_pa_s_kernel(
             )
             nc.vector.tensor_copy(out=repeated[:], in_=affine[:].unsqueeze(2).to_broadcast([P, 2, P]))
 
-        spread_ps = ps_cal.tile([P, 2, P], F32, tag="spread", name="spread_ps")
+        spread_ps = []
 
         def calib_spread_turn():
+            spread_ps.append(ps_cal.tile([P, 2, P], F32, tag="cal", name="spread_ps"))
             for c in range(2):
-                nc.tensor.transpose(out=spread_ps[:, c, :], in_=repeated[:, c, :], identity=ident_f32[:])
+                nc.tensor.transpose(
+                    out=spread_ps[0][:, c, :], in_=repeated[:, c, :], identity=ident_f32[:]
+                )
 
         def calib_spread_copy():
-            nc.vector.tensor_copy(out=spread[:], in_=spread_ps[:])
+            nc.vector.tensor_copy(out=spread[:], in_=spread_ps[0][:])
 
         z_ps = []
 
@@ -228,6 +239,8 @@ def tile_persistentcontrollayer_pa_s_kernel(
             )
         make_identity(nc, ident_f32[:])
         make_identity(nc, ident_bf[:])
+        for i in range(IDLE_MATMULS_AT_START):
+            idle_matmul()
         nc.gpsimd.memset(neg_half[:], -0.5)
         nc.vector.memset(logits[:, :, MODES : MODES + 1], 0.0)
 

@@ -21,7 +21,6 @@ PASSES = HIDDEN // K_PASS
 WR_TILES = RANK // P
 PAIRS = 2
 EPS = 1e-6
-IDLE_MATMULS_AT_START = 3
 
 FLOPS = 2 * BATCH * TOKENS * HIDDEN * RANK + 2 * BATCH * TOKENS * RANK * MODES
 
@@ -32,10 +31,7 @@ def tile_persistentcontrollayer_pa_s_kernel(
     nc = tc.nc
     with ExitStack() as ctx:
         keep = ctx.enter_context(tc.tile_pool(name="keep", bufs=1))
-        ps_turn = ctx.enter_context(tc.psum_pool(name="ps_turn", bufs=3))
-        ps_acc = ctx.enter_context(tc.psum_pool(name="ps_acc", bufs=1))
-        ps_cal = ctx.enter_context(tc.psum_pool(name="ps_cal", bufs=1))
-        ps_idle = ctx.enter_context(tc.psum_pool(name="ps_idle", bufs=1))
+        psum = ctx.enter_context(tc.psum_pool(name="psum", bufs=8))
         ctx.enter_context(tc.manual_schedule())
 
         scratch_sb = keep.tile([P, RANK], BF16, name="scratch_sb")
@@ -89,11 +85,6 @@ def tile_persistentcontrollayer_pa_s_kernel(
         inv_sum = keep.tile([P, BATCH], F32, name="inv_sum")
         routing = keep.tile([P, BATCH, MODES + 1], F32, name="routing")
 
-        idle_ps = ps_idle.tile([P, P], F32, name="idle_ps")
-
-        def idle_matmul():
-            nc.tensor.matmul(out=idle_ps[:], lhsT=ident_f32[:], rhs=ident_f32[:], start=True, stop=True)
-
         def inverse_root(values, c):
             nc.scalar.activation(out=squares[:], in_=values, func=ACT.Square, accum_out=sum_sq[c][:])
             nc.gpsimd.tensor_tensor(out=inv_root[c][:], in0=sum_sq[c][:], in1=neg_half[:], op=ALU.pow)
@@ -104,23 +95,23 @@ def tile_persistentcontrollayer_pa_s_kernel(
                 out=normed, in0=values, scalar1=inv_norm[c][:], scalar2=None, op0=ALU.mult
             )
 
-        def turn_rows(rows_sb, grouped_words):
+        def turn_rows(rows_sb, grouped, first_pass, passes):
             words = rows_sb[:].bitcast(F32)
-            turned = ps_turn.tile([P, PASSES, PAIRS, P], F32, tag="turn", name="turned")
-            for g in range(PASSES):
+            turned = psum.tile([P, passes, PAIRS, P], F32, tag="bank", name="turned")
+            for i in range(passes):
                 for u in range(PAIRS):
-                    first = (g * PAIRS + u) * P
+                    first = ((first_pass + i) * PAIRS + u) * P
                     nc.tensor.transpose(
-                        out=turned[:, g, u, :], in_=words[:, first : first + P], identity=ident_f32[:]
+                        out=turned[:, i, u, :], in_=words[:, first : first + P], identity=ident_f32[:]
                     )
-            idle_matmul()
-            nc.scalar.copy(out=grouped_words, in_=turned[:].rearrange("p g u r -> p g r u"))
+            grouped_words = grouped[:].bitcast(F32).rearrange("p (g r u) -> p g r u", g=PASSES, u=PAIRS)
+            nc.scalar.copy(
+                out=grouped_words[:, first_pass : first_pass + passes],
+                in_=turned[:].rearrange("p g u r -> p g r u"),
+            )
 
         def quantise_wr(t):
-            turn_rows(
-                wr_sb[t],
-                wr_grouped[t][:].bitcast(F32).rearrange("p (g r u) -> p g r u", g=PASSES, u=PAIRS),
-            )
+            turn_rows(wr_sb[t], wr_grouped[t], 0, PASSES)
             for g in range(PASSES):
                 first = (g * WR_TILES + t) * P
                 nc.vector.quantize_mx(
@@ -130,16 +121,16 @@ def tile_persistentcontrollayer_pa_s_kernel(
                 )
 
         def quantise_hs(b):
-            turn_rows(
-                hs_sb[b],
-                hs_grouped[b][:].bitcast(F32).rearrange("p (g r u) -> p g r u", g=PASSES, u=PAIRS),
-            )
-            nc.vector.quantize_mx(
-                out=hs_codes[b][:].bitcast(FP8X4), scales=hs_scales[b][:], in_=hs_grouped[b][:]
-            )
+            for g in range(PASSES):
+                turn_rows(hs_sb[b], hs_grouped[b], g, 1)
+                nc.vector.quantize_mx(
+                    out=hs_codes[b][:, g * TOKENS : (g + 1) * TOKENS].bitcast(FP8X4),
+                    scales=hs_scales[b][:, g * TOKENS : (g + 1) * TOKENS],
+                    in_=hs_grouped[b][:, g * TOKENS * PACK : (g + 1) * TOKENS * PACK],
+                )
 
         def turn_normed(normed, grouped):
-            turned = ps_turn.tile([P, PACK, P], BF16, tag="turn", name="turned_bf")
+            turned = psum.tile([P, PACK, P], BF16, tag="bank", name="turned_bf")
             for t in range(PACK):
                 nc.tensor.transpose(out=turned[:, t, :], in_=normed[:, t, :], identity=ident_bf[:])
             nc.scalar.copy(out=grouped, in_=turned[:].rearrange("p t r -> p r t"))
@@ -150,7 +141,7 @@ def tile_persistentcontrollayer_pa_s_kernel(
             )
 
         def calib_columns():
-            calib_ps = ps_cal.tile([P, P], BF16, tag="cal", name="calib_ps")
+            calib_ps = psum.tile([P, P], BF16, tag="bank", name="calib_ps")
             nc.tensor.transpose(out=calib_ps[:], in_=calib_rows[:], identity=ident_bf[:])
             nc.vector.tensor_copy(out=calib[:], in_=calib_ps[:, 0:3])
             nc.vector.tensor_scalar_max(out=std_floor[:], in0=calib[:, 1:2], scalar1=EPS)
@@ -164,7 +155,7 @@ def tile_persistentcontrollayer_pa_s_kernel(
         spread_ps = []
 
         def calib_spread_turn():
-            spread_ps.append(ps_cal.tile([P, 2, P], F32, tag="cal", name="spread_ps"))
+            spread_ps.append(psum.tile([P, 2, P], F32, tag="bank", name="spread_ps"))
             for c in range(2):
                 nc.tensor.transpose(
                     out=spread_ps[0][:, c, :], in_=repeated[:, c, :], identity=ident_f32[:]
@@ -176,7 +167,7 @@ def tile_persistentcontrollayer_pa_s_kernel(
         z_ps = []
 
         def first_matmul(b):
-            z_ps.append(ps_acc.tile([P, RANK], F32, tag="acc%d" % b, name="z_ps%d" % b))
+            z_ps.append(psum.tile([P, RANK], F32, tag="bank", name="z_ps%d" % b))
             for g in range(PASSES):
                 nc.tensor.matmul_mx(
                     out=z_ps[b][:],
@@ -191,8 +182,8 @@ def tile_persistentcontrollayer_pa_s_kernel(
         for_logits = []
 
         def second_matmul(b):
-            for_logits.append(ps_acc.tile([P, MODES], F32, tag="acc%d" % b, name="for_logits%d" % b))
-            for_store = ps_turn.tile([P, MODES], F32, tag="turn", name="for_store")
+            for_logits.append(psum.tile([P, MODES], F32, tag="bank", name="for_logits%d" % b))
+            for_store = psum.tile([P, MODES], F32, tag="bank", name="for_store")
             for bank in (for_logits[b], for_store):
                 nc.tensor.matmul_mx(
                     out=bank[:],
@@ -239,8 +230,6 @@ def tile_persistentcontrollayer_pa_s_kernel(
             )
         make_identity(nc, ident_f32[:])
         make_identity(nc, ident_bf[:])
-        for i in range(IDLE_MATMULS_AT_START):
-            idle_matmul()
         nc.gpsimd.memset(neg_half[:], -0.5)
         nc.vector.memset(logits[:, :, MODES : MODES + 1], 0.0)
 

@@ -40,7 +40,8 @@ def tile_persistentcontrollayer_pa_s_kernel(
         calib_rows = keep.tile([P, P], BF16, name="calib_rows")
         ident_bf = keep.tile([P, P], BF16, name="ident_bf")
         ident_f32 = keep.tile([P, P], F32, name="ident_f32")
-        neg_half = keep.tile([P, 1], F32, name="neg_half")
+        first_act = keep.tile([P, 1], F32, name="first_act")
+        zeros = keep.tile([P, P], F32, name="zeros")
         squares = keep.tile([P, RANK], BF16, name="squares")
         sum_sq = [keep.tile([P, 1], F32, name="sum_sq%d" % c) for c in range(1 + BATCH)]
         inv_root = [keep.tile([P, 1], F32, name="inv_root%d" % c) for c in range(1 + BATCH)]
@@ -48,7 +49,6 @@ def tile_persistentcontrollayer_pa_s_kernel(
         calib = keep.tile([P, 3], F32, name="calib")
         std_floor = keep.tile([P, 1], F32, name="std_floor")
         affine = keep.tile([P, 2], F32, name="affine")
-        repeated = keep.tile([P, 2, P], F32, name="repeated")
         spread = keep.tile([P, 2, P], F32, name="spread")
         s_norm = keep.tile([P, PACK, P], BF16, name="s_norm")
         s_grouped = keep.tile([P, MODES, PACK], BF16, name="s_grouped", align_bytes=64)
@@ -72,7 +72,7 @@ def tile_persistentcontrollayer_pa_s_kernel(
             keep.tile([P, PASSES * TOKENS], U8, name="hs_scales%d" % b, align_bytes=64)
             for b in range(BATCH)
         ]
-        z_norm = keep.tile([P, BATCH, PACK, P], BF16, name="z_norm")
+        inv_rows = [keep.tile([P, TOKENS], F32, name="inv_rows%d" % i) for i in range(BATCH)]
         z_grouped = keep.tile([P, BATCH, TOKENS, PACK], BF16, name="z_grouped", align_bytes=64)
         z_codes = keep.tile([P, BATCH, TOKENS], U32, name="z_codes", align_bytes=64)
         z_scales = keep.tile([P, BATCH, TOKENS], U8, name="z_scales", align_bytes=64)
@@ -87,7 +87,7 @@ def tile_persistentcontrollayer_pa_s_kernel(
 
         def inverse_root(values, c):
             nc.scalar.activation(out=squares[:], in_=values, func=ACT.Square, accum_out=sum_sq[c][:])
-            nc.gpsimd.tensor_tensor(out=inv_root[c][:], in0=sum_sq[c][:], in1=neg_half[:], op=ALU.pow)
+            nc.scalar.activation(out=inv_root[c][:], in_=sum_sq[c][:], func=ACT.Abs_reciprocal_sqrt)
 
         def normalise_rows(normed, values, c):
             nc.vector.tensor_scalar_min(out=inv_norm[c][:], in0=inv_root[c][:], scalar1=1.0 / EPS)
@@ -110,8 +110,13 @@ def tile_persistentcontrollayer_pa_s_kernel(
                 in_=turned[:].rearrange("p g u r -> p g r u"),
             )
 
+        def keep_clock():
+            unread = psum.tile([P, P], F32, tag="bank", name="unread")
+            nc.tensor.matmul(out=unread[:], lhsT=zeros[:], rhs=zeros[:], start=True, stop=True)
+
         def quantise_wr(t):
             turn_rows(wr_sb[t], wr_grouped[t], 0, PASSES)
+            keep_clock()
             for g in range(PASSES):
                 first = (g * WR_TILES + t) * P
                 nc.vector.quantize_mx(
@@ -133,7 +138,7 @@ def tile_persistentcontrollayer_pa_s_kernel(
             turned = psum.tile([P, PACK, P], BF16, tag="bank", name="turned_bf")
             for t in range(PACK):
                 nc.tensor.transpose(out=turned[:, t, :], in_=normed[:, t, :], identity=ident_bf[:])
-            nc.scalar.copy(out=grouped, in_=turned[:].rearrange("p t r -> p r t"))
+            nc.vector.tensor_copy(out=grouped, in_=turned[:].rearrange("p t r -> p r t"))
 
         def quantise_normed(grouped, codes, scales):
             nc.vector.quantize_mx(
@@ -150,7 +155,6 @@ def tile_persistentcontrollayer_pa_s_kernel(
                 out=affine[:, 1:2], in0=calib[:, 0:1], scalar1=affine[:, 0:1], scalar2=calib[:, 2:3],
                 op0=ALU.mult, op1=ALU.add,
             )
-            nc.vector.tensor_copy(out=repeated[:], in_=affine[:].unsqueeze(2).to_broadcast([P, 2, P]))
 
         spread_ps = []
 
@@ -158,7 +162,8 @@ def tile_persistentcontrollayer_pa_s_kernel(
             spread_ps.append(psum.tile([P, 2, P], F32, tag="bank", name="spread_ps"))
             for c in range(2):
                 nc.tensor.transpose(
-                    out=spread_ps[0][:, c, :], in_=repeated[:, c, :], identity=ident_f32[:]
+                    out=spread_ps[0][:, c, :], in_=affine[:, c : c + 1].to_broadcast([P, P]),
+                    identity=ident_f32[:],
                 )
 
         def calib_spread_copy():
@@ -179,6 +184,44 @@ def tile_persistentcontrollayer_pa_s_kernel(
                     stop=(g == PASSES - 1),
                 )
 
+        turned_z = []
+
+        def first_matmul_turned(b):
+            turned_z.append(psum.tile([P, PACK, TOKENS], F32, tag="bank", name="turned_z%d" % b))
+            for t in range(PACK):
+                for g in range(PASSES):
+                    first = (g * WR_TILES + t) * P
+                    nc.tensor.matmul_mx(
+                        out=turned_z[b][:, t, :],
+                        lhsT=wr_codes[:, first : first + P].bitcast(FP8X4),
+                        lhsT_scale=wr_scales[:, first : first + P],
+                        rhs=hs_codes[b][:, g * TOKENS : (g + 1) * TOKENS].bitcast(FP8X4),
+                        rhs_scale=hs_scales[b][:, g * TOKENS : (g + 1) * TOKENS],
+                        start=(g == 0),
+                        stop=(g == PASSES - 1),
+                    )
+
+        inv_ps = []
+
+        def spread_norms(b):
+            inv_ps.append(psum.tile([P, TOKENS], F32, tag="bank", name="inv_ps%d" % b))
+            nc.tensor.transpose(
+                out=inv_ps[b][:], in_=inv_root[1 + b][:].to_broadcast([P, P]), identity=ident_f32[:]
+            )
+
+        def copy_norms(b):
+            nc.vector.tensor_copy(out=inv_rows[b][:], in_=inv_ps[b][:])
+
+        def normalise_turned(b):
+            nc.vector.scalar_tensor_tensor(
+                out=z_grouped[:, b],
+                in0=inv_rows[b][:].unsqueeze(2).to_broadcast([P, TOKENS, PACK]),
+                scalar=1.0 / EPS,
+                in1=turned_z[b][:].rearrange("p t r -> p r t"),
+                op0=ALU.min,
+                op1=ALU.mult,
+            )
+
         for_logits = []
 
         def second_matmul(b):
@@ -194,10 +237,12 @@ def tile_persistentcontrollayer_pa_s_kernel(
             nc.scalar.copy(out=scores_sb[:, b, :], in_=for_store[:])
             nc.sync.dma_start(out=out_0[b], in_=scores_sb[:, b, :])
 
-        def exponentials(b):
+        def scale_scores(b):
             nc.vector.tensor_tensor(
                 out=scaled[:, b, :], in0=for_logits[b][:], in1=spread[:, 0, :], op=ALU.mult
             )
+
+        def exponentials(b):
             nc.vector.tensor_tensor(
                 out=logits[:, b, 0:MODES], in0=scaled[:, b, :], in1=spread[:, 1, :], op=ALU.subtract
             )
@@ -217,6 +262,9 @@ def tile_persistentcontrollayer_pa_s_kernel(
             )
             nc.sync.dma_start(out=out_1[b], in_=routing[:, b, :])
 
+        nc.vector.memset(zeros[:], 0.0)
+        for i in range(5):
+            keep_clock()
         nc.sync.dma_start(out=scratch_sb[:], in_=scratch)
         wr_rows = Wr.rearrange("(p t) k -> t p k", t=WR_TILES)
         for t in range(WR_TILES):
@@ -230,36 +278,51 @@ def tile_persistentcontrollayer_pa_s_kernel(
             )
         make_identity(nc, ident_f32[:])
         make_identity(nc, ident_bf[:])
-        nc.gpsimd.memset(neg_half[:], -0.5)
+        nc.vector.memset(first_act[:], 1.0)
+        nc.scalar.activation(out=first_act[:], in_=first_act[:], func=ACT.Abs_reciprocal_sqrt)
         nc.vector.memset(logits[:, :, MODES : MODES + 1], 0.0)
 
         inverse_root(scratch_sb[:], 0)
         normalise_rows(s_norm[:], scratch_sb[:].rearrange("m (p t) -> m t p", t=PACK), 0)
         quantise_wr(0)
         calib_columns()
-        for t in range(1, WR_TILES):
-            quantise_wr(t)
+        quantise_wr(1)
+        turn_normed(s_norm, s_grouped[:])
+        quantise_wr(2)
+        quantise_normed(s_grouped[:], s_codes[:], s_scales[:])
+        calib_spread_turn()
+        quantise_wr(3)
+        calib_spread_copy()
         for b in range(BATCH):
             quantise_hs(b)
+            if b == 0:
+                keep_clock()
+
         for b in range(BATCH):
             first_matmul(b)
             inverse_root(z_ps[b][:], 1 + b)
-
-        turn_normed(s_norm, s_grouped[:])
-        calib_spread_turn()
-
+        nc.scalar.activation(out=first_act[:], in_=first_act[:], func=ACT.Exp)
         for b in range(BATCH):
-            normalise_rows(z_norm[:, b].rearrange("k t p -> k (t p)"), z_ps[b][:], 1 + b)
-            turn_normed(z_norm[:, b], z_grouped[:, b])
-            if b == BATCH - 2:
-                calib_spread_copy()
-                quantise_normed(s_grouped[:], s_codes[:], s_scales[:])
+            first_matmul_turned(b)
+            spread_norms(b)
 
-        for b in range(BATCH):
-            quantise_normed(z_grouped[:, b], z_codes[:, b, :], z_scales[:, b, :])
-            second_matmul(b)
-            if b >= 1:
-                exponentials(b - 1)
-        exponentials(BATCH - 1)
+        copy_norms(0)
+        normalise_turned(0)
+        copy_norms(1)
+        quantise_normed(z_grouped[:, 0], z_codes[:, 0, :], z_scales[:, 0, :])
+        second_matmul(0)
+        normalise_turned(1)
+        copy_norms(2)
+        quantise_normed(z_grouped[:, 1], z_codes[:, 1, :], z_scales[:, 1, :])
+        second_matmul(1)
+        normalise_turned(2)
+        scale_scores(0)
+        quantise_normed(z_grouped[:, 2], z_codes[:, 2, :], z_scales[:, 2, :])
+        second_matmul(2)
+        exponentials(0)
+        scale_scores(1)
+        scale_scores(2)
+        exponentials(1)
+        exponentials(2)
         for b in range(BATCH):
             normalise(b)

@@ -95,7 +95,7 @@ def tile_persistentcontrollayer_pa_s_kernel(
                 out=normed, in0=values, scalar1=inv_norm[c][:], scalar2=None, op0=ALU.mult
             )
 
-        def turn_rows(rows_sb, grouped, first_pass, passes):
+        def turn_rows(rows_sb, first_pass, passes):
             words = rows_sb[:].bitcast(F32)
             turned = psum.tile([P, passes, PAIRS, P], F32, tag="bank", name="turned")
             for i in range(passes):
@@ -104,19 +104,16 @@ def tile_persistentcontrollayer_pa_s_kernel(
                     nc.tensor.transpose(
                         out=turned[:, i, u, :], in_=words[:, first : first + P], identity=ident_f32[:]
                     )
+            return turned
+
+        def regroup(copy, turned, grouped, first_pass, passes):
             grouped_words = grouped[:].bitcast(F32).rearrange("p (g r u) -> p g r u", g=PASSES, u=PAIRS)
-            nc.scalar.copy(
+            copy(
                 out=grouped_words[:, first_pass : first_pass + passes],
                 in_=turned[:].rearrange("p g u r -> p g r u"),
             )
 
-        def keep_clock():
-            unread = psum.tile([P, P], F32, tag="bank", name="unread")
-            nc.tensor.matmul(out=unread[:], lhsT=zeros[:], rhs=zeros[:], start=True, stop=True)
-
         def quantise_wr(t):
-            turn_rows(wr_sb[t], wr_grouped[t], 0, PASSES)
-            keep_clock()
             for g in range(PASSES):
                 first = (g * WR_TILES + t) * P
                 nc.vector.quantize_mx(
@@ -125,19 +122,24 @@ def tile_persistentcontrollayer_pa_s_kernel(
                     in_=wr_grouped[t][:, g * P * PACK : (g + 1) * P * PACK],
                 )
 
-        def quantise_hs(b):
-            for g in range(PASSES):
-                turn_rows(hs_sb[b], hs_grouped[b], g, 1)
-                nc.vector.quantize_mx(
-                    out=hs_codes[b][:, g * TOKENS : (g + 1) * TOKENS].bitcast(FP8X4),
-                    scales=hs_scales[b][:, g * TOKENS : (g + 1) * TOKENS],
-                    in_=hs_grouped[b][:, g * TOKENS * PACK : (g + 1) * TOKENS * PACK],
-                )
+        def quantise_hs(b, g):
+            nc.vector.quantize_mx(
+                out=hs_codes[b][:, g * TOKENS : (g + 1) * TOKENS].bitcast(FP8X4),
+                scales=hs_scales[b][:, g * TOKENS : (g + 1) * TOKENS],
+                in_=hs_grouped[b][:, g * TOKENS * PACK : (g + 1) * TOKENS * PACK],
+            )
 
-        def turn_normed(normed, grouped):
+        def keep_clock():
+            unread = psum.tile([P, P], F32, tag="bank", name="unread")
+            nc.tensor.matmul(out=unread[:], lhsT=zeros[:], rhs=zeros[:], start=True, stop=True)
+
+        def turn_normed(normed):
             turned = psum.tile([P, PACK, P], BF16, tag="bank", name="turned_bf")
             for t in range(PACK):
                 nc.tensor.transpose(out=turned[:, t, :], in_=normed[:, t, :], identity=ident_bf[:])
+            return turned
+
+        def regroup_normed(turned, grouped):
             nc.vector.tensor_copy(out=grouped, in_=turned[:].rearrange("p t r -> p r t"))
 
         def quantise_normed(grouped, codes, scales):
@@ -242,10 +244,12 @@ def tile_persistentcontrollayer_pa_s_kernel(
                 out=scaled[:, b, :], in0=for_logits[b][:], in1=spread[:, 0, :], op=ALU.mult
             )
 
-        def exponentials(b):
-            nc.vector.tensor_tensor(
+        def shift_scores(b, engine):
+            engine.tensor_tensor(
                 out=logits[:, b, 0:MODES], in0=scaled[:, b, :], in1=spread[:, 1, :], op=ALU.subtract
             )
+
+        def exponentials(b):
             nc.vector.tensor_reduce(
                 out=neg_max[:, b : b + 1], in_=logits[:, b, :], axis=AXIS.X, op=ALU.max, negate=True
             )
@@ -254,16 +258,21 @@ def tile_persistentcontrollayer_pa_s_kernel(
                 bias=neg_max[:, b : b + 1], scale=1.0, accum_out=exp_sum[:, b : b + 1],
             )
 
-        def normalise(b):
+        def normalise(b, on_scalar=False):
             nc.vector.reciprocal(out=inv_sum[:, b : b + 1], in_=exp_sum[:, b : b + 1])
-            nc.vector.tensor_scalar(
-                out=routing[:, b, :], in0=expd[:, b, :], scalar1=inv_sum[:, b : b + 1], scalar2=None,
-                op0=ALU.mult,
-            )
+            if on_scalar:
+                nc.scalar.activation(
+                    out=routing[:, b, :], in_=expd[:, b, :], func=ACT.Copy, scale=inv_sum[:, b : b + 1]
+                )
+            else:
+                nc.vector.tensor_scalar(
+                    out=routing[:, b, :], in0=expd[:, b, :], scalar1=inv_sum[:, b : b + 1], scalar2=None,
+                    op0=ALU.mult,
+                )
             nc.sync.dma_start(out=out_1[b], in_=routing[:, b, :])
 
         nc.vector.memset(zeros[:], 0.0)
-        for i in range(5):
+        for i in range(4):
             keep_clock()
         nc.sync.dma_start(out=scratch_sb[:], in_=scratch)
         wr_rows = Wr.rearrange("(p t) k -> t p k", t=WR_TILES)
@@ -282,47 +291,71 @@ def tile_persistentcontrollayer_pa_s_kernel(
         nc.scalar.activation(out=first_act[:], in_=first_act[:], func=ACT.Abs_reciprocal_sqrt)
         nc.vector.memset(logits[:, :, MODES : MODES + 1], 0.0)
 
+        calib_columns()
         inverse_root(scratch_sb[:], 0)
         normalise_rows(s_norm[:], scratch_sb[:].rearrange("m (p t) -> m t p", t=PACK), 0)
-        quantise_wr(0)
-        calib_columns()
-        quantise_wr(1)
-        turn_normed(s_norm, s_grouped[:])
-        quantise_wr(2)
-        quantise_normed(s_grouped[:], s_codes[:], s_scales[:])
-        calib_spread_turn()
-        quantise_wr(3)
-        calib_spread_copy()
-        for b in range(BATCH):
-            quantise_hs(b)
-            if b == 0:
+        for t in range(WR_TILES):
+            if t in (9,):
+                turned = turn_rows(wr_sb[t], 0, PASSES)
+                regroup(nc.vector.tensor_copy if (t, 0) in ((1,1),(3,1)) else nc.scalar.copy, turned, wr_grouped[t], 0, PASSES)
+            else:
+                for g in range(PASSES):
+                    turned = turn_rows(wr_sb[t], g, 1)
+                    regroup(nc.vector.tensor_copy if (t, g) in ((1,1),(3,1)) else nc.scalar.copy, turned, wr_grouped[t], g, 1)
+            if t in (1,2,3):
                 keep_clock()
-
+            quantise_wr(t)
         for b in range(BATCH):
-            first_matmul(b)
-            inverse_root(z_ps[b][:], 1 + b)
+            for g in range(PASSES):
+                turned = turn_rows(hs_sb[b], g, 1)
+                regroup(nc.vector.tensor_copy if (b, g) in (9,) else nc.scalar.copy, turned, hs_grouped[b], g, 1)
+                quantise_hs(b, g)
+            if b in (9,):
+                keep_clock()
+            if b == 1:
+                s_ps = turn_normed(s_norm)
+                calib_spread_turn()
+
+        first_matmul(0)
+        inverse_root(z_ps[0][:], 1)
+        first_matmul_turned(0)
+        regroup_normed(s_ps, s_grouped[:])
+        calib_spread_copy()
+        quantise_normed(s_grouped[:], s_codes[:], s_scales[:])
+        first_matmul(1)
+        inverse_root(z_ps[1][:], 2)
+        spread_norms(0)
+        first_matmul(2)
+        inverse_root(z_ps[2][:], 3)
         nc.scalar.activation(out=first_act[:], in_=first_act[:], func=ACT.Exp)
-        for b in range(BATCH):
-            first_matmul_turned(b)
-            spread_norms(b)
-
+        first_matmul_turned(1)
+        spread_norms(1)
+        first_matmul_turned(2)
+        spread_norms(2)
+        def normed(b):
+            quantise_normed(z_grouped[:, b], z_codes[:, b, :], z_scales[:, b, :])
+        v, g = nc.vector, nc.gpsimd
         copy_norms(0)
         normalise_turned(0)
-        copy_norms(1)
-        quantise_normed(z_grouped[:, 0], z_codes[:, 0, :], z_scales[:, 0, :])
+        normed(0)
         second_matmul(0)
+        copy_norms(1)
         normalise_turned(1)
         copy_norms(2)
-        quantise_normed(z_grouped[:, 1], z_codes[:, 1, :], z_scales[:, 1, :])
+        normed(1)
         second_matmul(1)
         normalise_turned(2)
         scale_scores(0)
-        quantise_normed(z_grouped[:, 2], z_codes[:, 2, :], z_scales[:, 2, :])
+        normed(2)
         second_matmul(2)
-        exponentials(0)
         scale_scores(1)
+        shift_scores(0,v)
+        shift_scores(1,v)
+        exponentials(0)
         scale_scores(2)
         exponentials(1)
+        shift_scores(2,v)
         exponentials(2)
-        for b in range(BATCH):
-            normalise(b)
+        normalise(0,True)
+        normalise(1,True)
+        normalise(2)

@@ -147,10 +147,14 @@ def tile_persistentcontrollayer_pa_s_kernel(
                 out=codes.bitcast(FP8X4), scales=scales, in_=grouped.rearrange("p r t -> p (r t)")
             )
 
+        calib_ps = []
+
+        def calib_turn():
+            calib_ps.append(psum.tile([P, P], BF16, tag="bank", name="calib_ps"))
+            nc.tensor.transpose(out=calib_ps[0][:], in_=calib_rows[:], identity=ident_bf[:])
+
         def calib_columns():
-            calib_ps = psum.tile([P, P], BF16, tag="bank", name="calib_ps")
-            nc.tensor.transpose(out=calib_ps[:], in_=calib_rows[:], identity=ident_bf[:])
-            nc.vector.tensor_copy(out=calib[:], in_=calib_ps[:, 0:3])
+            nc.vector.tensor_copy(out=calib[:], in_=calib_ps[0][:, 0:3])
             nc.vector.tensor_scalar_max(out=std_floor[:], in0=calib[:, 1:2], scalar1=EPS)
             nc.vector.reciprocal(out=affine[:, 0:1], in_=std_floor[:])
             nc.vector.tensor_scalar(
@@ -291,27 +295,24 @@ def tile_persistentcontrollayer_pa_s_kernel(
         nc.scalar.activation(out=first_act[:], in_=first_act[:], func=ACT.Abs_reciprocal_sqrt)
         nc.vector.memset(logits[:, :, MODES : MODES + 1], 0.0)
 
-        calib_columns()
         inverse_root(scratch_sb[:], 0)
         normalise_rows(s_norm[:], scratch_sb[:].rearrange("m (p t) -> m t p", t=PACK), 0)
         for t in range(WR_TILES):
-            if t in (9,):
-                turned = turn_rows(wr_sb[t], 0, PASSES)
-                regroup(nc.vector.tensor_copy if (t, 0) in ((1,1),(3,1)) else nc.scalar.copy, turned, wr_grouped[t], 0, PASSES)
-            else:
-                for g in range(PASSES):
-                    turned = turn_rows(wr_sb[t], g, 1)
-                    regroup(nc.vector.tensor_copy if (t, g) in ((1,1),(3,1)) else nc.scalar.copy, turned, wr_grouped[t], g, 1)
+            for g in range(PASSES):
+                turned = turn_rows(wr_sb[t], g, 1)
+                regroup(nc.vector.tensor_copy if (t, g) == (1, 1) else nc.scalar.copy, turned, wr_grouped[t], g, 1)
             if t in (1,2,3):
                 keep_clock()
+            if t == 1:
+                calib_turn()
             quantise_wr(t)
+            if t == 2:
+                calib_columns()
         for b in range(BATCH):
             for g in range(PASSES):
                 turned = turn_rows(hs_sb[b], g, 1)
-                regroup(nc.vector.tensor_copy if (b, g) in (9,) else nc.scalar.copy, turned, hs_grouped[b], g, 1)
+                regroup(nc.scalar.copy, turned, hs_grouped[b], g, 1)
                 quantise_hs(b, g)
-            if b in (9,):
-                keep_clock()
             if b == 1:
                 s_ps = turn_normed(s_norm)
                 calib_spread_turn()

@@ -42,10 +42,12 @@ def tile_persistentcontrollayer_pa_s_kernel(
         ident_f32 = keep.tile([P, P], F32, name="ident_f32")
         first_act = keep.tile([P, 1], F32, name="first_act")
         zeros = keep.tile([P, P], F32, name="zeros")
-        squares = keep.tile([P, RANK], BF16, name="squares")
+        squares = [keep.tile([P, RANK], BF16, name="squares%d" % c) for c in range(1 + BATCH)]
+        s_squares = keep.tile([P, RANK], BF16, name="s_squares")
         sum_sq = [keep.tile([P, 1], F32, name="sum_sq%d" % c) for c in range(1 + BATCH)]
         inv_root = [keep.tile([P, 1], F32, name="inv_root%d" % c) for c in range(1 + BATCH)]
         inv_norm = [keep.tile([P, 1], F32, name="inv_norm%d" % c) for c in range(1 + BATCH)]
+        z_norm = [keep.tile([P, PACK, P], BF16, name="z_norm%d" % b) for b in range(BATCH)]
         calib = keep.tile([P, 3], F32, name="calib")
         std_floor = keep.tile([P, 1], F32, name="std_floor")
         affine = keep.tile([P, 2], F32, name="affine")
@@ -85,11 +87,19 @@ def tile_persistentcontrollayer_pa_s_kernel(
         inv_sum = keep.tile([P, BATCH], F32, name="inv_sum")
         routing = keep.tile([P, BATCH, MODES + 1], F32, name="routing")
 
-        def inverse_root(values, c):
-            nc.scalar.activation(out=squares[:], in_=values, func=ACT.Square, accum_out=sum_sq[c][:])
+        def sum_squares(values, c):
+            nc.scalar.activation(out=squares[c][:], in_=values, func=ACT.Square, accum_out=sum_sq[c][:])
+
+        def sum_squares_scratch():
+            nc.vector.scalar_tensor_tensor(
+                out=s_squares[:], in0=scratch_sb[:], scalar=1.0, in1=scratch_sb[:],
+                op0=ALU.mult, op1=ALU.mult, accum_out=sum_sq[0][:],
+            )
+
+        def inverse_root(c=0):
             nc.scalar.activation(out=inv_root[c][:], in_=sum_sq[c][:], func=ACT.Abs_reciprocal_sqrt)
 
-        def normalise_rows(normed, values, c):
+        def normalise_rows(normed, values, c=0):
             nc.vector.tensor_scalar_min(out=inv_norm[c][:], in0=inv_root[c][:], scalar1=1.0 / EPS)
             nc.vector.tensor_scalar(
                 out=normed, in0=values, scalar1=inv_norm[c][:], scalar2=None, op0=ALU.mult
@@ -113,8 +123,8 @@ def tile_persistentcontrollayer_pa_s_kernel(
                 in_=turned[:].rearrange("p g u r -> p g r u"),
             )
 
-        def quantise_wr(t):
-            for g in range(PASSES):
+        def quantise_wr(t, gs=range(PASSES)):
+            for g in gs:
                 first = (g * WR_TILES + t) * P
                 nc.vector.quantize_mx(
                     out=wr_codes[:, first : first + P].bitcast(FP8X4),
@@ -122,11 +132,11 @@ def tile_persistentcontrollayer_pa_s_kernel(
                     in_=wr_grouped[t][:, g * P * PACK : (g + 1) * P * PACK],
                 )
 
-        def quantise_hs(b, g):
+        def quantise_hs(b, g, passes=1):
             nc.vector.quantize_mx(
-                out=hs_codes[b][:, g * TOKENS : (g + 1) * TOKENS].bitcast(FP8X4),
-                scales=hs_scales[b][:, g * TOKENS : (g + 1) * TOKENS],
-                in_=hs_grouped[b][:, g * TOKENS * PACK : (g + 1) * TOKENS * PACK],
+                out=hs_codes[b][:, g * TOKENS : (g + passes) * TOKENS].bitcast(FP8X4),
+                scales=hs_scales[b][:, g * TOKENS : (g + passes) * TOKENS],
+                in_=hs_grouped[b][:, g * TOKENS * PACK : (g + passes) * TOKENS * PACK],
             )
 
         def keep_clock():
@@ -139,8 +149,14 @@ def tile_persistentcontrollayer_pa_s_kernel(
                 nc.tensor.transpose(out=turned[:, t, :], in_=normed[:, t, :], identity=ident_bf[:])
             return turned
 
-        def regroup_normed(turned, grouped):
-            nc.vector.tensor_copy(out=grouped, in_=turned[:].rearrange("p t r -> p r t"))
+        def turn_scratch():
+            turned = psum.tile([P, PACK, P], F32, tag="bank", name="turned_s")
+            for t in range(PACK):
+                nc.tensor.matmul(out=turned[:, t, :], lhsT=s_norm[:, t, :], rhs=ident_bf[:], start=True, stop=True)
+            return turned
+
+        def regroup_normed(turned, grouped, copy=None):
+            (copy or nc.vector.tensor_copy)(out=grouped, in_=turned[:].rearrange("p t r -> p r t"))
 
         def quantise_normed(grouped, codes, scales):
             nc.vector.quantize_mx(
@@ -154,69 +170,87 @@ def tile_persistentcontrollayer_pa_s_kernel(
             nc.tensor.transpose(out=calib_ps[0][:], in_=calib_rows[:], identity=ident_bf[:])
 
         def calib_columns():
-            nc.vector.tensor_copy(out=calib[:], in_=calib_ps[0][:, 0:3])
-            nc.vector.tensor_scalar_max(out=std_floor[:], in0=calib[:, 1:2], scalar1=EPS)
-            nc.vector.reciprocal(out=affine[:, 0:1], in_=std_floor[:])
-            nc.vector.tensor_scalar(
-                out=affine[:, 1:2], in0=calib[:, 0:1], scalar1=affine[:, 0:1], scalar2=calib[:, 2:3],
-                op0=ALU.mult, op1=ALU.add,
-            )
+            for step in range(4):
+                calib_step(step)
+
+        def calib_step(step):
+            if step == 0:
+                nc.vector.tensor_copy(out=calib[:], in_=calib_ps[0][:, 0:3])
+            if step == 1:
+                nc.vector.tensor_scalar_max(out=std_floor[:], in0=calib[:, 1:2], scalar1=EPS)
+            if step == 2:
+                nc.vector.reciprocal(out=affine[:, 0:1], in_=std_floor[:])
+            if step == 3:
+                nc.vector.tensor_scalar(
+                    out=affine[:, 1:2], in0=calib[:, 0:1], scalar1=affine[:, 0:1], scalar2=calib[:, 2:3],
+                    op0=ALU.mult, op1=ALU.add,
+                )
 
         spread_ps = []
 
-        def calib_spread_turn():
+        def calib_spread_turn(as_matmul=False):
             spread_ps.append(psum.tile([P, 2, P], F32, tag="bank", name="spread_ps"))
             for c in range(2):
-                nc.tensor.transpose(
-                    out=spread_ps[0][:, c, :], in_=affine[:, c : c + 1].to_broadcast([P, P]),
-                    identity=ident_f32[:],
-                )
+                if as_matmul:
+                    nc.tensor.matmul(
+                        out=spread_ps[0][:, c, :], lhsT=affine[:, c : c + 1].to_broadcast([P, P]),
+                        rhs=ident_f32[:], start=True, stop=True,
+                    )
+                else:
+                    nc.tensor.transpose(
+                        out=spread_ps[0][:, c, :], in_=affine[:, c : c + 1].to_broadcast([P, P]),
+                        identity=ident_f32[:],
+                    )
 
         def calib_spread_copy():
             nc.vector.tensor_copy(out=spread[:], in_=spread_ps[0][:])
 
-        z_ps = []
+        z_ps = [None] * BATCH
+        turned_z = [None] * BATCH
 
-        def first_matmul(b):
-            z_ps.append(psum.tile([P, RANK], F32, tag="bank", name="z_ps%d" % b))
+        def open_banks(b):
+            z_ps[b] = psum.tile([P, RANK], F32, tag="bank", name="z_ps%d" % b)
+            turned_z[b] = psum.tile([P, PACK, TOKENS], F32, tag="bank", name="turned_z%d" % b)
+
+        def hs_operand(b, g):
+            cols = slice(g * TOKENS, (g + 1) * TOKENS)
+            return hs_codes[b][:, cols].bitcast(FP8X4), hs_scales[b][:, cols]
+
+        def wr_operand(g, first_tile, tiles):
+            cols = slice((g * WR_TILES + first_tile) * P, (g * WR_TILES + first_tile + tiles) * P)
+            return wr_codes[:, cols].bitcast(FP8X4), wr_scales[:, cols]
+
+        def first_matmul(b, first_tile=0, tiles=WR_TILES):
             for g in range(PASSES):
+                codes, scales = hs_operand(b, g)
+                wr_c, wr_s = wr_operand(g, first_tile, tiles)
                 nc.tensor.matmul_mx(
-                    out=z_ps[b][:],
-                    lhsT=hs_codes[b][:, g * TOKENS : (g + 1) * TOKENS].bitcast(FP8X4),
-                    lhsT_scale=hs_scales[b][:, g * TOKENS : (g + 1) * TOKENS],
-                    rhs=wr_codes[:, g * RANK : (g + 1) * RANK].bitcast(FP8X4),
-                    rhs_scale=wr_scales[:, g * RANK : (g + 1) * RANK],
-                    start=(g == 0),
-                    stop=(g == PASSES - 1),
+                    out=z_ps[b][:, first_tile * P : (first_tile + tiles) * P],
+                    lhsT=codes, lhsT_scale=scales, rhs=wr_c, rhs_scale=wr_s,
+                    start=(g == 0), stop=(g == PASSES - 1),
                 )
 
-        turned_z = []
-
-        def first_matmul_turned(b):
-            turned_z.append(psum.tile([P, PACK, TOKENS], F32, tag="bank", name="turned_z%d" % b))
-            for t in range(PACK):
+        def first_matmul_turned(b, tiles=range(WR_TILES)):
+            for t in tiles:
                 for g in range(PASSES):
-                    first = (g * WR_TILES + t) * P
+                    codes, scales = hs_operand(b, g)
+                    wr_c, wr_s = wr_operand(g, t, 1)
                     nc.tensor.matmul_mx(
                         out=turned_z[b][:, t, :],
-                        lhsT=wr_codes[:, first : first + P].bitcast(FP8X4),
-                        lhsT_scale=wr_scales[:, first : first + P],
-                        rhs=hs_codes[b][:, g * TOKENS : (g + 1) * TOKENS].bitcast(FP8X4),
-                        rhs_scale=hs_scales[b][:, g * TOKENS : (g + 1) * TOKENS],
-                        start=(g == 0),
-                        stop=(g == PASSES - 1),
+                        lhsT=wr_c, lhsT_scale=wr_s, rhs=codes, rhs_scale=scales,
+                        start=(g == 0), stop=(g == PASSES - 1),
                     )
 
-        inv_ps = []
+        sums_ps = {}
 
-        def spread_norms(b):
-            inv_ps.append(psum.tile([P, TOKENS], F32, tag="bank", name="inv_ps%d" % b))
+        def spread_sums(b):
+            sums_ps[b] = psum.tile([P, TOKENS], F32, tag="bank", name="sums_ps%d" % b)
             nc.tensor.transpose(
-                out=inv_ps[b][:], in_=inv_root[1 + b][:].to_broadcast([P, P]), identity=ident_f32[:]
+                out=sums_ps[b][:], in_=sum_sq[1 + b][:].to_broadcast([P, P]), identity=ident_f32[:]
             )
 
-        def copy_norms(b):
-            nc.vector.tensor_copy(out=inv_rows[b][:], in_=inv_ps[b][:])
+        def inverse_roots(b):
+            nc.scalar.activation(out=inv_rows[b][:], in_=sums_ps[b][:], func=ACT.Abs_reciprocal_sqrt)
 
         def normalise_turned(b):
             nc.vector.scalar_tensor_tensor(
@@ -241,7 +275,6 @@ def tile_persistentcontrollayer_pa_s_kernel(
                     start=True, stop=True,
                 )
             nc.scalar.copy(out=scores_sb[:, b, :], in_=for_store[:])
-            nc.sync.dma_start(out=out_0[b], in_=scores_sb[:, b, :])
 
         def scale_scores(b):
             nc.vector.tensor_tensor(
@@ -273,17 +306,19 @@ def tile_persistentcontrollayer_pa_s_kernel(
                     out=routing[:, b, :], in0=expd[:, b, :], scalar1=inv_sum[:, b : b + 1], scalar2=None,
                     op0=ALU.mult,
                 )
-            nc.sync.dma_start(out=out_1[b], in_=routing[:, b, :])
 
         nc.vector.memset(zeros[:], 0.0)
         for i in range(4):
             keep_clock()
         nc.sync.dma_start(out=scratch_sb[:], in_=scratch)
+        tokens = hidden_states.rearrange("b s k -> (b s) k").rearrange("(p c) k -> c p k", c=BATCH)
+        scores_rows = out_0.rearrange("b s m -> (b s) m").rearrange("(p c) m -> p c m", c=BATCH)
+        routing_rows = out_1.rearrange("b s m -> (b s) m").rearrange("(p c) m -> p c m", c=BATCH)
         wr_rows = Wr.rearrange("(p t) k -> t p k", t=WR_TILES)
         for t in range(WR_TILES):
             nc.sync.dma_start(out=wr_sb[t][:], in_=wr_rows[t])
         for b in range(BATCH):
-            nc.sync.dma_start(out=hs_sb[b][:], in_=hidden_states[b])
+            nc.sync.dma_start(out=hs_sb[b][:], in_=tokens[b])
         nc.vector.memset(calib_rows[:], 0.0)
         for row, vec in enumerate((calib_mean, calib_std, threshold)):
             nc.scalar.dma_start(
@@ -295,68 +330,102 @@ def tile_persistentcontrollayer_pa_s_kernel(
         nc.scalar.activation(out=first_act[:], in_=first_act[:], func=ACT.Abs_reciprocal_sqrt)
         nc.vector.memset(logits[:, :, MODES : MODES + 1], 0.0)
 
-        inverse_root(scratch_sb[:], 0)
-        normalise_rows(s_norm[:], scratch_sb[:].rearrange("m (p t) -> m t p", t=PACK), 0)
-        for t in range(WR_TILES):
-            for g in range(PASSES):
-                turned = turn_rows(wr_sb[t], g, 1)
-                regroup(nc.vector.tensor_copy if (t, g) == (1, 1) else nc.scalar.copy, turned, wr_grouped[t], g, 1)
-            if t in (1,2,3):
-                keep_clock()
-            if t == 1:
-                calib_turn()
-            quantise_wr(t)
-            if t == 2:
-                calib_columns()
-        for b in range(BATCH):
-            for g in range(PASSES):
-                turned = turn_rows(hs_sb[b], g, 1)
-                regroup(nc.scalar.copy, turned, hs_grouped[b], g, 1)
-                quantise_hs(b, g)
-            if b == 1:
-                s_ps = turn_normed(s_norm)
-                calib_spread_turn()
-
+        sum_squares(scratch_sb[:], 0)
+        inverse_root()
+        normalise_rows(s_norm[:], scratch_sb[:].rearrange("m (p t) -> m t p", t=PACK))
+        turned = turn_rows(wr_sb[0], 0, 1)
+        regroup(nc.scalar.copy, turned, wr_grouped[0], 0, 1)
+        turned = turn_rows(wr_sb[0], 1, 1)
+        regroup(nc.scalar.copy, turned, wr_grouped[0], 1, 1)
+        quantise_wr(0, [0])
+        quantise_wr(0, [1])
+        turned = turn_rows(wr_sb[1], 0, 1)
+        regroup(nc.scalar.copy, turned, wr_grouped[1], 0, 1)
+        turned = turn_rows(wr_sb[1], 1, 1)
+        regroup(nc.vector.tensor_copy, turned, wr_grouped[1], 1, 1)
+        calib_turn()
+        quantise_wr(1, [0])
+        calib_step(0)
+        quantise_wr(1, [1])
+        calib_step(1)
+        turned = turn_rows(wr_sb[2], 0, 1)
+        regroup(nc.scalar.copy, turned, wr_grouped[2], 0, 1)
+        turned = turn_rows(wr_sb[2], 1, 1)
+        regroup(nc.scalar.copy, turned, wr_grouped[2], 1, 1)
+        keep_clock()
+        keep_clock()
+        calib_step(2)
+        quantise_wr(2, [0])
+        calib_step(3)
+        quantise_wr(2, [1])
+        turned = turn_rows(wr_sb[3], 0, 1)
+        regroup(nc.scalar.copy, turned, wr_grouped[3], 0, 1)
+        turned = turn_rows(wr_sb[3], 1, 1)
+        regroup(nc.scalar.copy, turned, wr_grouped[3], 1, 1)
+        quantise_wr(3, [0])
+        quantise_wr(3, [1])
+        turned = turn_rows(hs_sb[0], 0, 1)
+        regroup(nc.scalar.copy, turned, hs_grouped[0], 0, 1)
+        turned = turn_rows(hs_sb[0], 1, 1)
+        regroup(nc.scalar.copy, turned, hs_grouped[0], 1, 1)
+        quantise_hs(0, 0)
+        quantise_hs(0, 1)
+        turned = turn_rows(hs_sb[1], 0, 1)
+        regroup(nc.scalar.copy, turned, hs_grouped[1], 0, 1)
+        turned = turn_rows(hs_sb[1], 1, 1)
+        regroup(nc.scalar.copy, turned, hs_grouped[1], 1, 1)
+        quantise_hs(1, 0)
+        quantise_hs(1, 1)
+        s_ps = turn_normed(s_norm)
+        calib_spread_turn()
+        turned = turn_rows(hs_sb[2], 0, 1)
+        regroup(nc.scalar.copy, turned, hs_grouped[2], 0, 1)
+        turned = turn_rows(hs_sb[2], 1, 1)
+        regroup(nc.scalar.copy, turned, hs_grouped[2], 1, 1)
+        quantise_hs(2, 0)
+        quantise_hs(2, 1)
+        open_banks(0)
         first_matmul(0)
-        inverse_root(z_ps[0][:], 1)
+        sum_squares(z_ps[0][:], 1)
         first_matmul_turned(0)
+        open_banks(1)
+        first_matmul(1)
+        sum_squares(z_ps[1][:], 2)
         regroup_normed(s_ps, s_grouped[:])
         calib_spread_copy()
         quantise_normed(s_grouped[:], s_codes[:], s_scales[:])
-        first_matmul(1)
-        inverse_root(z_ps[1][:], 2)
-        spread_norms(0)
+        spread_sums(0)
+        inverse_roots(0)
+        open_banks(2)
         first_matmul(2)
-        inverse_root(z_ps[2][:], 3)
-        nc.scalar.activation(out=first_act[:], in_=first_act[:], func=ACT.Exp)
+        sum_squares(z_ps[2][:], 3)
         first_matmul_turned(1)
-        spread_norms(1)
+        spread_sums(1)
+        inverse_roots(1)
         first_matmul_turned(2)
-        spread_norms(2)
-        def normed(b):
-            quantise_normed(z_grouped[:, b], z_codes[:, b, :], z_scales[:, b, :])
-        v, g = nc.vector, nc.gpsimd
-        copy_norms(0)
+        spread_sums(2)
+        inverse_roots(2)
+        nc.scalar.activation(out=first_act[:], in_=first_act[:], func=ACT.Exp)
         normalise_turned(0)
-        normed(0)
+        quantise_normed(z_grouped[:, 0], z_codes[:, 0, :], z_scales[:, 0, :])
         second_matmul(0)
-        copy_norms(1)
         normalise_turned(1)
-        copy_norms(2)
-        normed(1)
+        quantise_normed(z_grouped[:, 1], z_codes[:, 1, :], z_scales[:, 1, :])
         second_matmul(1)
         normalise_turned(2)
         scale_scores(0)
-        normed(2)
+        quantise_normed(z_grouped[:, 2], z_codes[:, 2, :], z_scales[:, 2, :])
         second_matmul(2)
         scale_scores(1)
-        shift_scores(0,v)
-        shift_scores(1,v)
+        shift_scores(0, nc.vector)
+        shift_scores(1, nc.vector)
         exponentials(0)
         scale_scores(2)
         exponentials(1)
-        shift_scores(2,v)
+        shift_scores(2, nc.vector)
         exponentials(2)
-        normalise(0,True)
-        normalise(1,True)
+        nc.sync.dma_start(out=scores_rows, in_=scores_sb[:])
+        normalise(0, True)
+        normalise(1, True)
         normalise(2)
+        nc.sync.dma_start(out=routing_rows, in_=routing[:])

@@ -35,13 +35,18 @@ def tile_persistentcontrollayer_pa_s_kernel(
         ctx.enter_context(tc.manual_schedule())
 
         scratch_sb = keep.tile([P, RANK], BF16, name="scratch_sb")
-        wr_sb = [keep.tile([P, HIDDEN], BF16, name="wr_sb%d" % t) for t in range(WR_TILES)]
-        hs_sb = [keep.tile([P, HIDDEN], BF16, name="hs_sb%d" % b) for b in range(BATCH)]
+        wr_all = keep.tile([P, WR_TILES, HIDDEN], BF16, name="wr_all")
+        hs_all = keep.tile([P, BATCH, HIDDEN], BF16, name="hs_all")
+        wr_sb = [wr_all[:, t, :] for t in range(WR_TILES)]
+        hs_sb = [hs_all[:, b, :] for b in range(BATCH)]
         calib_rows = keep.tile([P, P], BF16, name="calib_rows")
         ident_bf = keep.tile([P, P], BF16, name="ident_bf")
         ident_f32 = keep.tile([P, P], F32, name="ident_f32")
         first_act = keep.tile([P, 1], F32, name="first_act")
         zeros = keep.tile([P, P], F32, name="zeros")
+        ones = keep.tile([P, P], F32, name="ones")
+        sq = [keep.tile([P, PACK, TOKENS], F32, name="sq%d" % b) for b in range(BATCH)]
+        sq_pairs = [keep.tile([P, 2, TOKENS], F32, name="sq_pairs%d" % b) for b in range(BATCH)]
         squares = [keep.tile([P, RANK], BF16, name="squares%d" % c) for c in range(1 + BATCH)]
         s_squares = keep.tile([P, RANK], BF16, name="s_squares")
         sum_sq = [keep.tile([P, 1], F32, name="sum_sq%d" % c) for c in range(1 + BATCH)]
@@ -79,6 +84,7 @@ def tile_persistentcontrollayer_pa_s_kernel(
         z_codes = keep.tile([P, BATCH, TOKENS], U32, name="z_codes", align_bytes=64)
         z_scales = keep.tile([P, BATCH, TOKENS], U8, name="z_scales", align_bytes=64)
         scores_sb = keep.tile([P, BATCH, MODES], F32, name="scores_sb")
+        standard = keep.tile([P, BATCH, TOKENS], F32, name="standard")
         scaled = keep.tile([P, BATCH, MODES], F32, name="scaled")
         logits = keep.tile([P, BATCH, MODES + 1], F32, name="logits")
         neg_max = keep.tile([P, BATCH], F32, name="neg_max")
@@ -99,14 +105,18 @@ def tile_persistentcontrollayer_pa_s_kernel(
         def inverse_root(c=0):
             nc.scalar.activation(out=inv_root[c][:], in_=sum_sq[c][:], func=ACT.Abs_reciprocal_sqrt)
 
-        def normalise_rows(normed, values, c=0):
+        def clamp(c):
             nc.vector.tensor_scalar_min(out=inv_norm[c][:], in0=inv_root[c][:], scalar1=1.0 / EPS)
+
+        def normalise_rows(normed, values, c=0, clamped=False):
+            if not clamped:
+                clamp(c)
             nc.vector.tensor_scalar(
                 out=normed, in0=values, scalar1=inv_norm[c][:], scalar2=None, op0=ALU.mult
             )
 
         def turn_rows(rows_sb, first_pass, passes):
-            words = rows_sb[:].bitcast(F32)
+            words = rows_sb.bitcast(F32)
             turned = psum.tile([P, passes, PAIRS, P], F32, tag="bank", name="turned")
             for i in range(passes):
                 for u in range(PAIRS):
@@ -241,6 +251,19 @@ def tile_persistentcontrollayer_pa_s_kernel(
                         start=(g == 0), stop=(g == PASSES - 1),
                     )
 
+        def square_turned(b):
+            nc.scalar.activation(out=sq[b][:], in_=turned_z[b][:], func=ACT.Square)
+
+        def add_pairs(b, engine):
+            engine.tensor_tensor(out=sq_pairs[b][:], in0=sq[b][:, 0:2], in1=sq[b][:, 2:4], op=ALU.add)
+
+        def sum_ranks(b):
+            sums_ps[b] = psum.tile([P, TOKENS], F32, tag="bank", name="sums_ps%d" % b)
+            for i in range(2):
+                nc.tensor.matmul(
+                    out=sums_ps[b][:], lhsT=ones[:], rhs=sq_pairs[b][:, i, :], start=(i == 0), stop=(i == 1)
+                )
+
         sums_ps = {}
 
         def spread_sums(b):
@@ -276,6 +299,45 @@ def tile_persistentcontrollayer_pa_s_kernel(
                 )
             nc.scalar.copy(out=scores_sb[:, b, :], in_=for_store[:])
 
+        logits_ps = {}
+
+        def second_matmul_both(b):
+            for_logits.append(psum.tile([P, TOKENS], F32, tag="bank", name="for_logits%d" % b))
+            for_store = psum.tile([P, MODES], F32, tag="bank", name="for_store")
+            z_operand = dict(codes=z_codes[:, b, :].bitcast(FP8X4), scales=z_scales[:, b, :])
+            s_operand = dict(codes=s_codes[:].bitcast(FP8X4), scales=s_scales[:])
+            for bank, left, right in (
+                (for_logits[b], s_operand, z_operand), (for_store, z_operand, s_operand),
+            ):
+                nc.tensor.matmul_mx(
+                    out=bank[:], lhsT=left["codes"], lhsT_scale=left["scales"],
+                    rhs=right["codes"], rhs_scale=right["scales"], start=True, stop=True,
+                )
+            nc.scalar.copy(out=scores_sb[:, b, :], in_=for_store[:])
+
+        def standardise(b):
+            nc.vector.tensor_scalar(
+                out=standard[:, b, :], in0=for_logits[b][:], scalar1=affine[:, 0:1], scalar2=affine[:, 1:2],
+                op0=ALU.mult, op1=ALU.subtract,
+            )
+
+        def open_logits(b):
+            logits_ps[b] = psum.tile([P, 2, MODES], F32, tag="bank", name="logits_ps%d" % b)
+            nc.tensor.transpose(out=logits_ps[b][:, 1, :], in_=zeros[:], identity=ident_f32[:])
+
+        def turn_logits(b):
+            nc.tensor.transpose(out=logits_ps[b][:, 0, :], in_=standard[:, b, :], identity=ident_f32[:])
+
+        def exponentials_turned(b):
+            values = logits_ps[b][:].rearrange("p c m -> p (c m)")[:, 0 : MODES + 1]
+            nc.vector.tensor_reduce(
+                out=neg_max[:, b : b + 1], in_=values, axis=AXIS.X, op=ALU.max, negate=True
+            )
+            nc.scalar.activation(
+                out=expd[:, b, :], in_=values, func=ACT.Exp,
+                bias=neg_max[:, b : b + 1], scale=1.0, accum_out=exp_sum[:, b : b + 1],
+            )
+
         def scale_scores(b):
             nc.vector.tensor_tensor(
                 out=scaled[:, b, :], in0=for_logits[b][:], in1=spread[:, 0, :], op=ALU.mult
@@ -308,17 +370,22 @@ def tile_persistentcontrollayer_pa_s_kernel(
                 )
 
         nc.vector.memset(zeros[:], 0.0)
+        nc.vector.memset(ones[:], 1.0)
         for i in range(4):
             keep_clock()
-        nc.sync.dma_start(out=scratch_sb[:], in_=scratch)
-        tokens = hidden_states.rearrange("b s k -> (b s) k").rearrange("(p c) k -> c p k", c=BATCH)
+        tokens = hidden_states.rearrange("b s k -> (b s) k").rearrange("(p c) k -> p c k", c=BATCH)
         scores_rows = out_0.rearrange("b s m -> (b s) m").rearrange("(p c) m -> p c m", c=BATCH)
         routing_rows = out_1.rearrange("b s m -> (b s) m").rearrange("(p c) m -> p c m", c=BATCH)
-        wr_rows = Wr.rearrange("(p t) k -> t p k", t=WR_TILES)
-        for t in range(WR_TILES):
-            nc.sync.dma_start(out=wr_sb[t][:], in_=wr_rows[t])
-        for b in range(BATCH):
-            nc.sync.dma_start(out=hs_sb[b][:], in_=tokens[b])
+        wr_rows = Wr.rearrange("(p t) k -> p t k", t=WR_TILES)
+        nc.sync.dma_start(out=wr_all[:, 0, 0 * K_PASS : 1 * K_PASS], in_=wr_rows[:, 0, 0 * K_PASS : 1 * K_PASS])
+        nc.sync.dma_start(out=wr_all[:, 0, 1 * K_PASS : 2 * K_PASS], in_=wr_rows[:, 0, 1 * K_PASS : 2 * K_PASS])
+        nc.sync.dma_start(out=wr_all[:, 1 : 2, :], in_=wr_rows[:, 1 : 2, :])
+        nc.sync.dma_start(out=scratch_sb[:], in_=scratch)
+        nc.sync.dma_start(out=wr_all[:, 2 : 3, :], in_=wr_rows[:, 2 : 3, :])
+        nc.sync.dma_start(out=wr_all[:, 3 : 4, :], in_=wr_rows[:, 3 : 4, :])
+        nc.sync.dma_start(out=hs_all[:, 0 : 1, :], in_=tokens[:, 0 : 1, :])
+        nc.sync.dma_start(out=hs_all[:, 1 : 2, :], in_=tokens[:, 1 : 2, :])
+        nc.sync.dma_start(out=hs_all[:, 2 : 3, :], in_=tokens[:, 2 : 3, :])
         nc.vector.memset(calib_rows[:], 0.0)
         for row, vec in enumerate((calib_mean, calib_std, threshold)):
             nc.scalar.dma_start(
@@ -330,19 +397,21 @@ def tile_persistentcontrollayer_pa_s_kernel(
         nc.scalar.activation(out=first_act[:], in_=first_act[:], func=ACT.Abs_reciprocal_sqrt)
         nc.vector.memset(logits[:, :, MODES : MODES + 1], 0.0)
 
-        sum_squares(scratch_sb[:], 0)
-        inverse_root()
-        normalise_rows(s_norm[:], scratch_sb[:].rearrange("m (p t) -> m t p", t=PACK))
         turned = turn_rows(wr_sb[0], 0, 1)
         regroup(nc.scalar.copy, turned, wr_grouped[0], 0, 1)
         turned = turn_rows(wr_sb[0], 1, 1)
         regroup(nc.scalar.copy, turned, wr_grouped[0], 1, 1)
-        quantise_wr(0, [0])
-        quantise_wr(0, [1])
+        sum_squares_scratch()
+        inverse_root(0)
         turned = turn_rows(wr_sb[1], 0, 1)
         regroup(nc.scalar.copy, turned, wr_grouped[1], 0, 1)
         turned = turn_rows(wr_sb[1], 1, 1)
-        regroup(nc.vector.tensor_copy, turned, wr_grouped[1], 1, 1)
+        regroup(nc.scalar.copy, turned, wr_grouped[1], 1, 1)
+        keep_clock()
+        keep_clock()
+        quantise_wr(0, [0])
+        normalise_rows(s_norm[:], scratch_sb[:].rearrange("m (p t) -> m t p", t=PACK))
+        quantise_wr(0, [1])
         calib_turn()
         quantise_wr(1, [0])
         calib_step(0)
@@ -351,9 +420,7 @@ def tile_persistentcontrollayer_pa_s_kernel(
         turned = turn_rows(wr_sb[2], 0, 1)
         regroup(nc.scalar.copy, turned, wr_grouped[2], 0, 1)
         turned = turn_rows(wr_sb[2], 1, 1)
-        regroup(nc.scalar.copy, turned, wr_grouped[2], 1, 1)
-        keep_clock()
-        keep_clock()
+        regroup(nc.vector.tensor_copy, turned, wr_grouped[2], 1, 1)
         calib_step(2)
         quantise_wr(2, [0])
         calib_step(3)
@@ -364,6 +431,7 @@ def tile_persistentcontrollayer_pa_s_kernel(
         regroup(nc.scalar.copy, turned, wr_grouped[3], 1, 1)
         quantise_wr(3, [0])
         quantise_wr(3, [1])
+        keep_clock()
         turned = turn_rows(hs_sb[0], 0, 1)
         regroup(nc.scalar.copy, turned, hs_grouped[0], 0, 1)
         turned = turn_rows(hs_sb[0], 1, 1)
@@ -377,7 +445,6 @@ def tile_persistentcontrollayer_pa_s_kernel(
         quantise_hs(1, 0)
         quantise_hs(1, 1)
         s_ps = turn_normed(s_norm)
-        calib_spread_turn()
         turned = turn_rows(hs_sb[2], 0, 1)
         regroup(nc.scalar.copy, turned, hs_grouped[2], 0, 1)
         turned = turn_rows(hs_sb[2], 1, 1)
@@ -392,7 +459,6 @@ def tile_persistentcontrollayer_pa_s_kernel(
         first_matmul(1)
         sum_squares(z_ps[1][:], 2)
         regroup_normed(s_ps, s_grouped[:])
-        calib_spread_copy()
         quantise_normed(s_grouped[:], s_codes[:], s_scales[:])
         spread_sums(0)
         inverse_roots(0)
@@ -408,22 +474,25 @@ def tile_persistentcontrollayer_pa_s_kernel(
         nc.scalar.activation(out=first_act[:], in_=first_act[:], func=ACT.Exp)
         normalise_turned(0)
         quantise_normed(z_grouped[:, 0], z_codes[:, 0, :], z_scales[:, 0, :])
-        second_matmul(0)
+        second_matmul_both(0)
+        open_logits(0)
         normalise_turned(1)
         quantise_normed(z_grouped[:, 1], z_codes[:, 1, :], z_scales[:, 1, :])
-        second_matmul(1)
+        second_matmul_both(1)
+        open_logits(1)
         normalise_turned(2)
-        scale_scores(0)
+        standardise(0)
+        turn_logits(0)
         quantise_normed(z_grouped[:, 2], z_codes[:, 2, :], z_scales[:, 2, :])
-        second_matmul(2)
-        scale_scores(1)
-        shift_scores(0, nc.vector)
-        shift_scores(1, nc.vector)
-        exponentials(0)
-        scale_scores(2)
-        exponentials(1)
-        shift_scores(2, nc.vector)
-        exponentials(2)
+        second_matmul_both(2)
+        open_logits(2)
+        standardise(1)
+        turn_logits(1)
+        exponentials_turned(0)
+        standardise(2)
+        turn_logits(2)
+        exponentials_turned(1)
+        exponentials_turned(2)
         nc.sync.dma_start(out=scores_rows, in_=scores_sb[:])
         normalise(0, True)
         normalise(1, True)

@@ -44,9 +44,6 @@ def tile_persistentcontrollayer_pa_s_kernel(
         ident_f32 = keep.tile([P, P], F32, name="ident_f32")
         first_act = keep.tile([P, 1], F32, name="first_act")
         zeros = keep.tile([P, P], F32, name="zeros")
-        ones = keep.tile([P, P], F32, name="ones")
-        sq = [keep.tile([P, PACK, TOKENS], F32, name="sq%d" % b) for b in range(BATCH)]
-        sq_pairs = [keep.tile([P, 2, TOKENS], F32, name="sq_pairs%d" % b) for b in range(BATCH)]
         squares = [keep.tile([P, RANK], BF16, name="squares%d" % c) for c in range(1 + BATCH)]
         s_squares = keep.tile([P, RANK], BF16, name="s_squares")
         sum_sq = [keep.tile([P, 1], F32, name="sum_sq%d" % c) for c in range(1 + BATCH)]
@@ -151,7 +148,7 @@ def tile_persistentcontrollayer_pa_s_kernel(
 
         def keep_clock():
             unread = psum.tile([P, P], F32, tag="bank", name="unread")
-            nc.tensor.matmul(out=unread[:], lhsT=zeros[:], rhs=zeros[:], start=True, stop=True)
+            nc.tensor.matmul(out=unread[:], lhsT=ident_f32[:], rhs=ident_f32[:], start=True, stop=True)
 
         def turn_normed(normed):
             turned = psum.tile([P, PACK, P], BF16, tag="bank", name="turned_bf")
@@ -250,19 +247,6 @@ def tile_persistentcontrollayer_pa_s_kernel(
                         lhsT=wr_c, lhsT_scale=wr_s, rhs=codes, rhs_scale=scales,
                         start=(g == 0), stop=(g == PASSES - 1),
                     )
-
-        def square_turned(b):
-            nc.scalar.activation(out=sq[b][:], in_=turned_z[b][:], func=ACT.Square)
-
-        def add_pairs(b, engine):
-            engine.tensor_tensor(out=sq_pairs[b][:], in0=sq[b][:, 0:2], in1=sq[b][:, 2:4], op=ALU.add)
-
-        def sum_ranks(b):
-            sums_ps[b] = psum.tile([P, TOKENS], F32, tag="bank", name="sums_ps%d" % b)
-            for i in range(2):
-                nc.tensor.matmul(
-                    out=sums_ps[b][:], lhsT=ones[:], rhs=sq_pairs[b][:, i, :], start=(i == 0), stop=(i == 1)
-                )
 
         sums_ps = {}
 
@@ -369,8 +353,8 @@ def tile_persistentcontrollayer_pa_s_kernel(
                     op0=ALU.mult,
                 )
 
+        make_identity(nc, ident_f32[:])
         nc.vector.memset(zeros[:], 0.0)
-        nc.vector.memset(ones[:], 1.0)
         for i in range(4):
             keep_clock()
         tokens = hidden_states.rearrange("b s k -> (b s) k").rearrange("(p c) k -> p c k", c=BATCH)
@@ -391,7 +375,6 @@ def tile_persistentcontrollayer_pa_s_kernel(
             nc.scalar.dma_start(
                 out=calib_rows[row : row + 1, :], in_=vec.rearrange("(o m) -> o m", o=1)
             )
-        make_identity(nc, ident_f32[:])
         make_identity(nc, ident_bf[:])
         nc.vector.memset(first_act[:], 1.0)
         nc.scalar.activation(out=first_act[:], in_=first_act[:], func=ACT.Abs_reciprocal_sqrt)

@@ -44,6 +44,7 @@ def tile_persistentcontrollayer_pa_s_kernel(
         ident_f32 = keep.tile([P, P], F32, name="ident_f32")
         first_act = keep.tile([P, 1], F32, name="first_act")
         zeros = keep.tile([P, P], F32, name="zeros")
+        numbers = keep.tile([P, P], F32, name="numbers")
         squares = [keep.tile([P, RANK], BF16, name="squares%d" % c) for c in range(1 + BATCH)]
         s_squares = keep.tile([P, RANK], BF16, name="s_squares")
         sum_sq = [keep.tile([P, 1], F32, name="sum_sq%d" % c) for c in range(1 + BATCH)]
@@ -148,7 +149,7 @@ def tile_persistentcontrollayer_pa_s_kernel(
 
         def keep_clock():
             unread = psum.tile([P, P], F32, tag="bank", name="unread")
-            nc.tensor.matmul(out=unread[:], lhsT=ident_f32[:], rhs=ident_f32[:], start=True, stop=True)
+            nc.tensor.matmul(out=unread[:], lhsT=numbers[:], rhs=numbers[:], start=True, stop=True)
 
         def turn_normed(normed):
             turned = psum.tile([P, PACK, P], BF16, tag="bank", name="turned_bf")
@@ -353,6 +354,9 @@ def tile_persistentcontrollayer_pa_s_kernel(
                     op0=ALU.mult,
                 )
 
+        nc.gpsimd.iota(
+            numbers[:], pattern=[[1, P]], base=1, channel_multiplier=1, allow_small_or_imprecise_dtypes=True
+        )
         make_identity(nc, ident_f32[:])
         nc.vector.memset(zeros[:], 0.0)
         for i in range(4):
@@ -391,22 +395,16 @@ def tile_persistentcontrollayer_pa_s_kernel(
         turned = turn_rows(wr_sb[1], 1, 1)
         regroup(nc.scalar.copy, turned, wr_grouped[1], 1, 1)
         keep_clock()
-        keep_clock()
         quantise_wr(0, [0])
         normalise_rows(s_norm[:], scratch_sb[:].rearrange("m (p t) -> m t p", t=PACK))
         quantise_wr(0, [1])
-        calib_turn()
         quantise_wr(1, [0])
-        calib_step(0)
         quantise_wr(1, [1])
-        calib_step(1)
         turned = turn_rows(wr_sb[2], 0, 1)
         regroup(nc.scalar.copy, turned, wr_grouped[2], 0, 1)
         turned = turn_rows(wr_sb[2], 1, 1)
-        regroup(nc.vector.tensor_copy, turned, wr_grouped[2], 1, 1)
-        calib_step(2)
+        regroup(nc.scalar.copy, turned, wr_grouped[2], 1, 1)
         quantise_wr(2, [0])
-        calib_step(3)
         quantise_wr(2, [1])
         turned = turn_rows(wr_sb[3], 0, 1)
         regroup(nc.scalar.copy, turned, wr_grouped[3], 0, 1)
@@ -421,6 +419,7 @@ def tile_persistentcontrollayer_pa_s_kernel(
         regroup(nc.scalar.copy, turned, hs_grouped[0], 1, 1)
         quantise_hs(0, 0)
         quantise_hs(0, 1)
+        keep_clock()
         turned = turn_rows(hs_sb[1], 0, 1)
         regroup(nc.scalar.copy, turned, hs_grouped[1], 0, 1)
         turned = turn_rows(hs_sb[1], 1, 1)
@@ -428,6 +427,7 @@ def tile_persistentcontrollayer_pa_s_kernel(
         quantise_hs(1, 0)
         quantise_hs(1, 1)
         s_ps = turn_normed(s_norm)
+        calib_turn()
         turned = turn_rows(hs_sb[2], 0, 1)
         regroup(nc.scalar.copy, turned, hs_grouped[2], 0, 1)
         turned = turn_rows(hs_sb[2], 1, 1)
@@ -437,20 +437,24 @@ def tile_persistentcontrollayer_pa_s_kernel(
         open_banks(0)
         first_matmul(0)
         sum_squares(z_ps[0][:], 1)
-        first_matmul_turned(0)
         open_banks(1)
         first_matmul(1)
         sum_squares(z_ps[1][:], 2)
+        first_matmul_turned(0)
+        calib_step(0)
         regroup_normed(s_ps, s_grouped[:])
+        calib_step(1)
         quantise_normed(s_grouped[:], s_codes[:], s_scales[:])
+        calib_step(2)
+        calib_step(3)
         spread_sums(0)
         inverse_roots(0)
         open_banks(2)
         first_matmul(2)
         sum_squares(z_ps[2][:], 3)
-        first_matmul_turned(1)
         spread_sums(1)
         inverse_roots(1)
+        first_matmul_turned(1)
         first_matmul_turned(2)
         spread_sums(2)
         inverse_roots(2)

@@ -270,6 +270,21 @@ def tile_persistentcontrollayer_pa_s_kernel(
                 op1=ALU.mult,
             )
 
+        def normalise_half(b, h):
+            tok = slice(h * TOKENS // 2, (h + 1) * TOKENS // 2)
+            nc.vector.scalar_tensor_tensor(
+                out=z_grouped[:, b, tok],
+                in0=inv_rows[b][:, tok].unsqueeze(2).to_broadcast([P, TOKENS // 2, PACK]),
+                scalar=1.0 / EPS,
+                in1=turned_z[b][:, :, tok].rearrange("p t r -> p r t"),
+                op0=ALU.min,
+                op1=ALU.mult,
+            )
+
+        def quantise_half(b, h):
+            tok = slice(h * TOKENS // 2, (h + 1) * TOKENS // 2)
+            quantise_normed(z_grouped[:, b, tok], z_codes[:, b, tok], z_scales[:, b, tok])
+
         for_logits = []
 
         def second_matmul(b):
@@ -395,6 +410,7 @@ def tile_persistentcontrollayer_pa_s_kernel(
         turned = turn_rows(wr_sb[1], 1, 1)
         regroup(nc.scalar.copy, turned, wr_grouped[1], 1, 1)
         keep_clock()
+        keep_clock()
         quantise_wr(0, [0])
         normalise_rows(s_norm[:], scratch_sb[:].rearrange("m (p t) -> m t p", t=PACK))
         quantise_wr(0, [1])
@@ -413,13 +429,13 @@ def tile_persistentcontrollayer_pa_s_kernel(
         quantise_wr(3, [0])
         quantise_wr(3, [1])
         keep_clock()
+        keep_clock()
         turned = turn_rows(hs_sb[0], 0, 1)
         regroup(nc.scalar.copy, turned, hs_grouped[0], 0, 1)
         turned = turn_rows(hs_sb[0], 1, 1)
         regroup(nc.scalar.copy, turned, hs_grouped[0], 1, 1)
         quantise_hs(0, 0)
         quantise_hs(0, 1)
-        keep_clock()
         turned = turn_rows(hs_sb[1], 0, 1)
         regroup(nc.scalar.copy, turned, hs_grouped[1], 0, 1)
         turned = turn_rows(hs_sb[1], 1, 1)
@@ -483,5 +499,6 @@ def tile_persistentcontrollayer_pa_s_kernel(
         nc.sync.dma_start(out=scores_rows, in_=scores_sb[:])
         normalise(0, True)
         normalise(1, True)
+        nc.sync.dma_start(out=routing_rows[:, 0:2, :], in_=routing[:, 0:2, :])
         normalise(2)
-        nc.sync.dma_start(out=routing_rows, in_=routing[:])
+        nc.sync.dma_start(out=routing_rows[:, 2:3, :], in_=routing[:, 2:3, :])

from contextlib import ExitStack

import concourse.mybir as mybir
from concourse.masks import make_identity

F32 = mybir.dt.float32
BF16 = mybir.dt.bfloat16
U32 = mybir.dt.uint32
U8 = mybir.dt.uint8
FP8X4 = mybir.dt.float8_e4m3fn_x4
ALU = mybir.AluOpType
ACT = mybir.ActivationFunctionType
AXIS = mybir.AxisListType

P = 128
PACK = 4
K_PASS = P * PACK
BATCH, TOKENS, HIDDEN = 3, 128, 1024
RANK, MODES = 512, 128
PASSES = HIDDEN // K_PASS
WR_TILES = RANK // P
PAIRS = 2
EPS = 1e-6

FLOPS = 2 * BATCH * TOKENS * HIDDEN * RANK + 2 * BATCH * TOKENS * RANK * MODES


def tile_persistentcontrollayer_pa_s_kernel(
    tc, hidden_states, Wr, scratch, threshold, calib_mean, calib_std, out_0, out_1
):
    nc = tc.nc
    with ExitStack() as ctx:
        keep = ctx.enter_context(tc.tile_pool(name="keep", bufs=1))
        psum = ctx.enter_context(tc.psum_pool(name="psum", bufs=8))
        ctx.enter_context(tc.manual_schedule())

        scratch_sb = keep.tile([P, RANK], BF16, name="scratch_sb")
        wr_all = keep.tile([P, WR_TILES, HIDDEN], BF16, name="wr_all")
        hs_all = keep.tile([P, BATCH, HIDDEN], BF16, name="hs_all")
        wr_sb = [wr_all[:, t, :] for t in range(WR_TILES)]
        hs_sb = [hs_all[:, b, :] for b in range(BATCH)]
        calib_rows = keep.tile([P, P], BF16, name="calib_rows")
        ident_bf = keep.tile([P, P], BF16, name="ident_bf")
        ident_f32 = keep.tile([P, P], F32, name="ident_f32")
        first_act = keep.tile([P, 1], F32, name="first_act")
        zeros = keep.tile([P, P], F32, name="zeros")
        numbers = keep.tile([P, P], F32, name="numbers")
        squares = [keep.tile([P, RANK], BF16, name="squares%d" % c) for c in range(1 + BATCH)]
        s_squares = keep.tile([P, RANK], BF16, name="s_squares")
        sum_sq = [keep.tile([P, 1], F32, name="sum_sq%d" % c) for c in range(1 + BATCH)]
        inv_root = [keep.tile([P, 1], F32, name="inv_root%d" % c) for c in range(1 + BATCH)]
        inv_norm = [keep.tile([P, 1], F32, name="inv_norm%d" % c) for c in range(1 + BATCH)]
        z_norm = [keep.tile([P, PACK, P], BF16, name="z_norm%d" % b) for b in range(BATCH)]
        calib = keep.tile([P, 3], F32, name="calib")
        std_floor = keep.tile([P, 1], F32, name="std_floor")
        affine = keep.tile([P, 2], F32, name="affine")
        spread = keep.tile([P, 2, P], F32, name="spread")
        s_norm = keep.tile([P, PACK, P], BF16, name="s_norm")
        s_grouped = keep.tile([P, MODES, PACK], BF16, name="s_grouped", align_bytes=64)
        s_codes = keep.tile([P, MODES], U32, name="s_codes", align_bytes=64)
        s_scales = keep.tile([P, MODES], U8, name="s_scales", align_bytes=64)
        wr_grouped = [
            keep.tile([P, PASSES * P * PACK], BF16, name="wr_grouped%d" % t, align_bytes=64)
            for t in range(WR_TILES)
        ]
        wr_codes = keep.tile([P, PASSES * RANK], U32, name="wr_codes", align_bytes=64)
        wr_scales = keep.tile([P, PASSES * RANK], U8, name="wr_scales", align_bytes=64)
        hs_grouped = [
            keep.tile([P, PASSES * TOKENS * PACK], BF16, name="hs_grouped%d" % b, align_bytes=64)
            for b in range(BATCH)
        ]
        hs_codes = [
            keep.tile([P, PASSES * TOKENS], U32, name="hs_codes%d" % b, align_bytes=64)
            for b in range(BATCH)
        ]
        hs_scales = [
            keep.tile([P, PASSES * TOKENS], U8, name="hs_scales%d" % b, align_bytes=64)
            for b in range(BATCH)
        ]
        inv_rows = [keep.tile([P, TOKENS], F32, name="inv_rows%d" % i) for i in range(BATCH)]
        z_grouped = keep.tile([P, BATCH, TOKENS, PACK], BF16, name="z_grouped", align_bytes=64)
        z_codes = keep.tile([P, BATCH, TOKENS], U32, name="z_codes", align_bytes=64)
        z_scales = keep.tile([P, BATCH, TOKENS], U8, name="z_scales", align_bytes=64)
        scores_sb = keep.tile([P, BATCH, MODES], F32, name="scores_sb")
        standard = keep.tile([P, BATCH, TOKENS], F32, name="standard")
        scaled = keep.tile([P, BATCH, MODES], F32, name="scaled")
        logits = keep.tile([P, BATCH, MODES + 1], F32, name="logits")
        neg_max = keep.tile([P, BATCH], F32, name="neg_max")
        expd = keep.tile([P, BATCH, MODES + 1], F32, name="expd")
        exp_sum = keep.tile([P, BATCH], F32, name="exp_sum")
        inv_sum = keep.tile([P, BATCH], F32, name="inv_sum")
        routing = keep.tile([P, BATCH, MODES + 1], F32, name="routing")

        def sum_squares(values, c):
            nc.scalar.activation(out=squares[c][:], in_=values, func=ACT.Square, accum_out=sum_sq[c][:])

        def sum_squares_scratch():
            nc.vector.scalar_tensor_tensor(
                out=s_squares[:], in0=scratch_sb[:], scalar=1.0, in1=scratch_sb[:],
                op0=ALU.mult, op1=ALU.mult, accum_out=sum_sq[0][:],
            )

        def inverse_root(c=0):
            nc.scalar.activation(out=inv_root[c][:], in_=sum_sq[c][:], func=ACT.Abs_reciprocal_sqrt)

        def clamp(c):
            nc.vector.tensor_scalar_min(out=inv_norm[c][:], in0=inv_root[c][:], scalar1=1.0 / EPS)

        def normalise_rows(normed, values, c=0, clamped=False):
            if not clamped:
                clamp(c)
            nc.vector.tensor_scalar(
                out=normed, in0=values, scalar1=inv_norm[c][:], scalar2=None, op0=ALU.mult
            )

        def turn_rows(rows_sb, first_pass, passes):
            words = rows_sb.bitcast(F32)
            turned = psum.tile([P, passes, PAIRS, P], F32, tag="bank", name="turned")
            for i in range(passes):
                for u in range(PAIRS):
                    first = ((first_pass + i) * PAIRS + u) * P
                    nc.tensor.transpose(
                        out=turned[:, i, u, :], in_=words[:, first : first + P], identity=ident_f32[:]
                    )
            return turned

        def regroup(copy, turned, grouped, first_pass, passes):
            grouped_words = grouped[:].bitcast(F32).rearrange("p (g r u) -> p g r u", g=PASSES, u=PAIRS)
            copy(
                out=grouped_words[:, first_pass : first_pass + passes],
                in_=turned[:].rearrange("p g u r -> p g r u"),
            )

        def quantise_wr(t, gs=range(PASSES)):
            for g in gs:
                first = (g * WR_TILES + t) * P
                nc.vector.quantize_mx(
                    out=wr_codes[:, first : first + P].bitcast(FP8X4),
                    scales=wr_scales[:, first : first + P],
                    in_=wr_grouped[t][:, g * P * PACK : (g + 1) * P * PACK],
                )

        def quantise_hs(b, g, passes=1):
            nc.vector.quantize_mx(
                out=hs_codes[b][:, g * TOKENS : (g + passes) * TOKENS].bitcast(FP8X4),
                scales=hs_scales[b][:, g * TOKENS : (g + passes) * TOKENS],
                in_=hs_grouped[b][:, g * TOKENS * PACK : (g + passes) * TOKENS * PACK],
            )

        def keep_clock():
            unread = psum.tile([P, P], F32, tag="bank", name="unread")
            nc.tensor.matmul(out=unread[:], lhsT=numbers[:], rhs=numbers[:], start=True, stop=True)

        def turn_normed(normed):
            turned = psum.tile([P, PACK, P], BF16, tag="bank", name="turned_bf")
            for t in range(PACK):
                nc.tensor.transpose(out=turned[:, t, :], in_=normed[:, t, :], identity=ident_bf[:])
            return turned

        def turn_scratch():
            turned = psum.tile([P, PACK, P], F32, tag="bank", name="turned_s")
            for t in range(PACK):
                nc.tensor.matmul(out=turned[:, t, :], lhsT=s_norm[:, t, :], rhs=ident_bf[:], start=True, stop=True)
            return turned

        def regroup_normed(turned, grouped, copy=None):
            (copy or nc.vector.tensor_copy)(out=grouped, in_=turned[:].rearrange("p t r -> p r t"))

        def quantise_normed(grouped, codes, scales):
            nc.vector.quantize_mx(
                out=codes.bitcast(FP8X4), scales=scales, in_=grouped.rearrange("p r t -> p (r t)")
            )

        calib_ps = []

        def calib_turn():
            calib_ps.append(psum.tile([P, P], BF16, tag="bank", name="calib_ps"))
            nc.tensor.transpose(out=calib_ps[0][:], in_=calib_rows[:], identity=ident_bf[:])

        def calib_columns():
            for step in range(4):
                calib_step(step)

        def calib_step(step):
            if step == 0:
                nc.vector.tensor_copy(out=calib[:], in_=calib_ps[0][:, 0:3])
            if step == 1:
                nc.vector.tensor_scalar_max(out=std_floor[:], in0=calib[:, 1:2], scalar1=EPS)
            if step == 2:
                nc.vector.reciprocal(out=affine[:, 0:1], in_=std_floor[:])
            if step == 3:
                nc.vector.tensor_scalar(
                    out=affine[:, 1:2], in0=calib[:, 0:1], scalar1=affine[:, 0:1], scalar2=calib[:, 2:3],
                    op0=ALU.mult, op1=ALU.add,
                )

        spread_ps = []

        def calib_spread_turn(as_matmul=False):
            spread_ps.append(psum.tile([P, 2, P], F32, tag="bank", name="spread_ps"))
            for c in range(2):
                if as_matmul:
                    nc.tensor.matmul(
                        out=spread_ps[0][:, c, :], lhsT=affine[:, c : c + 1].to_broadcast([P, P]),
                        rhs=ident_f32[:], start=True, stop=True,
                    )
                else:
                    nc.tensor.transpose(
                        out=spread_ps[0][:, c, :], in_=affine[:, c : c + 1].to_broadcast([P, P]),
                        identity=ident_f32[:],
                    )

        def calib_spread_copy():
            nc.vector.tensor_copy(out=spread[:], in_=spread_ps[0][:])

        z_ps = [None] * BATCH
        turned_z = [None] * BATCH

        def open_banks(b):
            z_ps[b] = psum.tile([P, RANK], F32, tag="bank", name="z_ps%d" % b)
            turned_z[b] = psum.tile([P, PACK, TOKENS], F32, tag="bank", name="turned_z%d" % b)

        def hs_operand(b, g):
            cols = slice(g * TOKENS, (g + 1) * TOKENS)
            return hs_codes[b][:, cols].bitcast(FP8X4), hs_scales[b][:, cols]

        def wr_operand(g, first_tile, tiles):
            cols = slice((g * WR_TILES + first_tile) * P, (g * WR_TILES + first_tile + tiles) * P)
            return wr_codes[:, cols].bitcast(FP8X4), wr_scales[:, cols]

        def first_matmul(b, first_tile=0, tiles=WR_TILES):
            for g in range(PASSES):
                codes, scales = hs_operand(b, g)
                wr_c, wr_s = wr_operand(g, first_tile, tiles)
                nc.tensor.matmul_mx(
                    out=z_ps[b][:, first_tile * P : (first_tile + tiles) * P],
                    lhsT=codes, lhsT_scale=scales, rhs=wr_c, rhs_scale=wr_s,
                    start=(g == 0), stop=(g == PASSES - 1),
                )

        def first_matmul_turned(b, tiles=range(WR_TILES)):
            for t in tiles:
                for g in range(PASSES):
                    codes, scales = hs_operand(b, g)
                    wr_c, wr_s = wr_operand(g, t, 1)
                    nc.tensor.matmul_mx(
                        out=turned_z[b][:, t, :],
                        lhsT=wr_c, lhsT_scale=wr_s, rhs=codes, rhs_scale=scales,
                        start=(g == 0), stop=(g == PASSES - 1),
                    )

        sums_ps = {}

        def spread_sums(b):
            sums_ps[b] = psum.tile([P, TOKENS], F32, tag="bank", name="sums_ps%d" % b)
            nc.tensor.transpose(
                out=sums_ps[b][:], in_=sum_sq[1 + b][:].to_broadcast([P, P]), identity=ident_f32[:]
            )

        def inverse_roots(b):
            nc.scalar.activation(out=inv_rows[b][:], in_=sums_ps[b][:], func=ACT.Abs_reciprocal_sqrt)

        def normalise_turned(b):
            nc.vector.scalar_tensor_tensor(
                out=z_grouped[:, b],
                in0=inv_rows[b][:].unsqueeze(2).to_broadcast([P, TOKENS, PACK]),
                scalar=1.0 / EPS,
                in1=turned_z[b][:].rearrange("p t r -> p r t"),
                op0=ALU.min,
                op1=ALU.mult,
            )

        def normalise_half(b, h):
            tok = slice(h * TOKENS // 2, (h + 1) * TOKENS // 2)
            nc.vector.scalar_tensor_tensor(
                out=z_grouped[:, b, tok],
                in0=inv_rows[b][:, tok].unsqueeze(2).to_broadcast([P, TOKENS // 2, PACK]),
                scalar=1.0 / EPS,
                in1=turned_z[b][:, :, tok].rearrange("p t r -> p r t"),
                op0=ALU.min,
                op1=ALU.mult,
            )

        def quantise_half(b, h):
            tok = slice(h * TOKENS // 2, (h + 1) * TOKENS // 2)
            quantise_normed(z_grouped[:, b, tok], z_codes[:, b, tok], z_scales[:, b, tok])

        for_logits = []

        def second_matmul(b):
            for_logits.append(psum.tile([P, MODES], F32, tag="bank", name="for_logits%d" % b))
            for_store = psum.tile([P, MODES], F32, tag="bank", name="for_store")
            for bank in (for_logits[b], for_store):
                nc.tensor.matmul_mx(
                    out=bank[:],
                    lhsT=z_codes[:, b, :].bitcast(FP8X4), lhsT_scale=z_scales[:, b, :],
                    rhs=s_codes[:].bitcast(FP8X4), rhs_scale=s_scales[:],
                    start=True, stop=True,
                )
            nc.scalar.copy(out=scores_sb[:, b, :], in_=for_store[:])

        logits_ps = {}

        def second_matmul_both(b):
            for_logits.append(psum.tile([P, TOKENS], F32, tag="bank", name="for_logits%d" % b))
            for_store = psum.tile([P, MODES], F32, tag="bank", name="for_store")
            z_operand = dict(codes=z_codes[:, b, :].bitcast(FP8X4), scales=z_scales[:, b, :])
            s_operand = dict(codes=s_codes[:].bitcast(FP8X4), scales=s_scales[:])
            for bank, left, right in (
                (for_logits[b], s_operand, z_operand), (for_store, z_operand, s_operand),
            ):
                nc.tensor.matmul_mx(
                    out=bank[:], lhsT=left["codes"], lhsT_scale=left["scales"],
                    rhs=right["codes"], rhs_scale=right["scales"], start=True, stop=True,
                )
            nc.scalar.copy(out=scores_sb[:, b, :], in_=for_store[:])

        def standardise(b):
            nc.vector.tensor_scalar(
                out=standard[:, b, :], in0=for_logits[b][:], scalar1=affine[:, 0:1], scalar2=affine[:, 1:2],
                op0=ALU.mult, op1=ALU.subtract,
            )

        def open_logits(b):
            logits_ps[b] = psum.tile([P, 2, MODES], F32, tag="bank", name="logits_ps%d" % b)
            nc.tensor.transpose(out=logits_ps[b][:, 1, :], in_=zeros[:], identity=ident_f32[:])

        def turn_logits(b):
            nc.tensor.transpose(out=logits_ps[b][:, 0, :], in_=standard[:, b, :], identity=ident_f32[:])

        def exponentials_turned(b):
            values = logits_ps[b][:].rearrange("p c m -> p (c m)")[:, 0 : MODES + 1]
            nc.vector.tensor_reduce(
                out=neg_max[:, b : b + 1], in_=values, axis=AXIS.X, op=ALU.max, negate=True
            )
            nc.scalar.activation(
                out=expd[:, b, :], in_=values, func=ACT.Exp,
                bias=neg_max[:, b : b + 1], scale=1.0, accum_out=exp_sum[:, b : b + 1],
            )

        def scale_scores(b):
            nc.vector.tensor_tensor(
                out=scaled[:, b, :], in0=for_logits[b][:], in1=spread[:, 0, :], op=ALU.mult
            )

        def shift_scores(b, engine):
            engine.tensor_tensor(
                out=logits[:, b, 0:MODES], in0=scaled[:, b, :], in1=spread[:, 1, :], op=ALU.subtract
            )

        def exponentials(b):
            nc.vector.tensor_reduce(
                out=neg_max[:, b : b + 1], in_=logits[:, b, :], axis=AXIS.X, op=ALU.max, negate=True
            )
            nc.scalar.activation(
                out=expd[:, b, :], in_=logits[:, b, :], func=ACT.Exp,
                bias=neg_max[:, b : b + 1], scale=1.0, accum_out=exp_sum[:, b : b + 1],
            )

        def normalise(b, on_scalar=False):
            nc.vector.reciprocal(out=inv_sum[:, b : b + 1], in_=exp_sum[:, b : b + 1])
            if on_scalar:
                nc.scalar.activation(
                    out=routing[:, b, :], in_=expd[:, b, :], func=ACT.Copy, scale=inv_sum[:, b : b + 1]
                )
            else:
                nc.vector.tensor_scalar(
                    out=routing[:, b, :], in0=expd[:, b, :], scalar1=inv_sum[:, b : b + 1], scalar2=None,
                    op0=ALU.mult,
                )

        nc.gpsimd.iota(
            numbers[:], pattern=[[1, P]], base=1, channel_multiplier=1, allow_small_or_imprecise_dtypes=True
        )
        make_identity(nc, ident_f32[:])
        nc.vector.memset(zeros[:], 0.0)
        for i in range(4):
            keep_clock()
        tokens = hidden_states.rearrange("b s k -> (b s) k").rearrange("(p c) k -> p c k", c=BATCH)
        scores_rows = out_0.rearrange("b s m -> (b s) m").rearrange("(p c) m -> p c m", c=BATCH)
        routing_rows = out_1.rearrange("b s m -> (b s) m").rearrange("(p c) m -> p c m", c=BATCH)
        wr_rows = Wr.rearrange("(p t) k -> p t k", t=WR_TILES)
        nc.sync.dma_start(out=wr_all[:, 0, 0 * K_PASS : 1 * K_PASS], in_=wr_rows[:, 0, 0 * K_PASS : 1 * K_PASS])
        nc.sync.dma_start(out=wr_all[:, 0, 1 * K_PASS : 2 * K_PASS], in_=wr_rows[:, 0, 1 * K_PASS : 2 * K_PASS])
        nc.sync.dma_start(out=wr_all[:, 1 : 2, :], in_=wr_rows[:, 1 : 2, :])
        nc.sync.dma_start(out=scratch_sb[:], in_=scratch)
        nc.sync.dma_start(out=wr_all[:, 2 : 3, :], in_=wr_rows[:, 2 : 3, :])
        nc.sync.dma_start(out=wr_all[:, 3 : 4, :], in_=wr_rows[:, 3 : 4, :])
        nc.sync.dma_start(out=hs_all[:, 0 : 1, :], in_=tokens[:, 0 : 1, :])
        nc.sync.dma_start(out=hs_all[:, 1 : 2, :], in_=tokens[:, 1 : 2, :])
        nc.sync.dma_start(out=hs_all[:, 2 : 3, :], in_=tokens[:, 2 : 3, :])
        nc.vector.memset(calib_rows[:], 0.0)
        for row, vec in enumerate((calib_mean, calib_std, threshold)):
            nc.scalar.dma_start(
                out=calib_rows[row : row + 1, :], in_=vec.rearrange("(o m) -> o m", o=1)
            )
        make_identity(nc, ident_bf[:])
        nc.vector.memset(first_act[:], 1.0)
        nc.scalar.activation(out=first_act[:], in_=first_act[:], func=ACT.Abs_reciprocal_sqrt)
        nc.vector.memset(logits[:, :, MODES : MODES + 1], 0.0)

        turned = turn_rows(wr_sb[0], 0, 1)
        regroup(nc.scalar.copy, turned, wr_grouped[0], 0, 1)
        turned = turn_rows(wr_sb[0], 1, 1)
        regroup(nc.scalar.copy, turned, wr_grouped[0], 1, 1)
        sum_squares_scratch()
        inverse_root(0)
        turned = turn_rows(wr_sb[1], 0, 1)
        regroup(nc.scalar.copy, turned, wr_grouped[1], 0, 1)
        turned = turn_rows(wr_sb[1], 1, 1)
        regroup(nc.scalar.copy, turned, wr_grouped[1], 1, 1)
        keep_clock()
        keep_clock()
        quantise_wr(0, [0])
        normalise_rows(s_norm[:], scratch_sb[:].rearrange("m (p t) -> m t p", t=PACK))
        quantise_wr(0, [1])
        quantise_wr(1, [0])
        quantise_wr(1, [1])
        turned = turn_rows(wr_sb[2], 0, 1)
        regroup(nc.scalar.copy, turned, wr_grouped[2], 0, 1)
        turned = turn_rows(wr_sb[2], 1, 1)
        regroup(nc.scalar.copy, turned, wr_grouped[2], 1, 1)
        quantise_wr(2, [0])
        quantise_wr(2, [1])
        turned = turn_rows(wr_sb[3], 0, 1)
        regroup(nc.scalar.copy, turned, wr_grouped[3], 0, 1)
        turned = turn_rows(wr_sb[3], 1, 1)
        regroup(nc.scalar.copy, turned, wr_grouped[3], 1, 1)
        quantise_wr(3, [0])
        quantise_wr(3, [1])
        keep_clock()
        keep_clock()
        turned = turn_rows(hs_sb[0], 0, 1)
        regroup(nc.scalar.copy, turned, hs_grouped[0], 0, 1)
        turned = turn_rows(hs_sb[0], 1, 1)
        regroup(nc.scalar.copy, turned, hs_grouped[0], 1, 1)
        quantise_hs(0, 0)
        quantise_hs(0, 1)
        turned = turn_rows(hs_sb[1], 0, 1)
        regroup(nc.scalar.copy, turned, hs_grouped[1], 0, 1)
        turned = turn_rows(hs_sb[1], 1, 1)
        regroup(nc.scalar.copy, turned, hs_grouped[1], 1, 1)
        quantise_hs(1, 0)
        quantise_hs(1, 1)
        s_ps = turn_normed(s_norm)
        calib_turn()
        turned = turn_rows(hs_sb[2], 0, 1)
        regroup(nc.scalar.copy, turned, hs_grouped[2], 0, 1)
        turned = turn_rows(hs_sb[2], 1, 1)
        regroup(nc.scalar.copy, turned, hs_grouped[2], 1, 1)
        quantise_hs(2, 0)
        quantise_hs(2, 1)
        open_banks(0)
        first_matmul(0)
        sum_squares(z_ps[0][:], 1)
        open_banks(1)
        first_matmul(1)
        sum_squares(z_ps[1][:], 2)
        first_matmul_turned(0)
        calib_step(0)
        regroup_normed(s_ps, s_grouped[:])
        calib_step(1)
        quantise_normed(s_grouped[:], s_codes[:], s_scales[:])
        calib_step(2)
        calib_step(3)
        spread_sums(0)
        inverse_roots(0)
        open_banks(2)
        first_matmul(2)
        sum_squares(z_ps[2][:], 3)
        spread_sums(1)
        inverse_roots(1)
        first_matmul_turned(1)
        first_matmul_turned(2)
        spread_sums(2)
        inverse_roots(2)
        nc.scalar.activation(out=first_act[:], in_=first_act[:], func=ACT.Exp)
        normalise_turned(0)
        quantise_normed(z_grouped[:, 0], z_codes[:, 0, :], z_scales[:, 0, :])
        second_matmul_both(0)
        open_logits(0)
        normalise_turned(1)
        quantise_normed(z_grouped[:, 1], z_codes[:, 1, :], z_scales[:, 1, :])
        second_matmul_both(1)
        open_logits(1)
        normalise_turned(2)
        standardise(0)
        turn_logits(0)
        quantise_normed(z_grouped[:, 2], z_codes[:, 2, :], z_scales[:, 2, :])
        second_matmul_both(2)
        open_logits(2)
        standardise(1)
        turn_logits(1)
        exponentials_turned(0)
        standardise(2)
        turn_logits(2)
        exponentials_turned(1)
        exponentials_turned(2)
        nc.sync.dma_start(out=scores_rows, in_=scores_sb[:])
        normalise(0, True)
        normalise(1, True)
        nc.sync.dma_start(out=routing_rows[:, 0:2, :], in_=routing[:, 0:2, :])
        normalise(2)
        nc.sync.dma_start(out=routing_rows[:, 2:3, :], in_=routing[:, 2:3, :])
